import numpy as np
import ml_dtypes


def mxq(x, axis, fmt="e4m3"):
    dtype, down = {"e4m3": (ml_dtypes.float8_e4m3fn, 7), "e5m2": (ml_dtypes.float8_e5m2, 14)}[fmt]
    v = np.moveaxis(np.asarray(x, np.float32).astype(ml_dtypes.bfloat16).astype(np.float64), axis, -1)
    blocks = v.reshape(v.shape[:-1] + (-1, 32))
    amax = np.abs(blocks).max(-1, keepdims=True)
    byte = np.maximum(np.where(amax > 0, np.frexp(amax)[1] - 1 + 127, 0) - down, 1)
    scale = np.exp2(byte - 127.0)
    codes = (blocks / scale).astype(np.float32).astype(dtype).astype(np.float64)
    return np.moveaxis((codes * scale).reshape(v.shape), -1, axis)


WIDE = False


def mx_kscale(k):
    if not WIDE:
        return np.ones(k)
    levels = np.array([10, -10, 5, -5, 0])
    a = np.random.permutation(np.resize(levels, k // 512 * 4)).reshape(k // 512, 4)
    idx = np.arange(k)
    return np.exp2(a[idx // 512, idx % 128 // 32])


BF16 = ml_dtypes.bfloat16


def bf(x):
    return np.asarray(x, np.float32).astype(BF16)


def f64(x):
    return np.asarray(x).astype(np.float64)


S, HID, H, KV, D, WINDOW, QB = 1024, 1024, 8, 4, 256, 512, 512
NQ, NK = H * D, KV * D
EPS = 1e-6
ROPE_THETA = 10000.0


def rms_norm(x, w):
    var = np.mean(x * x, axis=-1, keepdims=True)
    return x * (1.0 / np.sqrt(var + EPS)) * (1.0 + w)


def rotate_half(x):
    x1, x2 = np.split(x, 2, axis=-1)
    return np.concatenate([-x2, x1], axis=-1)


def apply_rope(x, cos, sin):
    return x * cos[:, None, :] + rotate_half(x) * sin[:, None, :]


def setup_inputs():
    s = mx_kscale(HID)
    inv_freq = 1.0 / ROPE_THETA ** (np.arange(0, D, 2) / D)
    freqs = np.outer(np.arange(S), inv_freq)
    emb = np.concatenate([freqs, freqs], -1)
    return {"hidden_states": bf(np.random.standard_normal((S, HID)) * s),
            "w_qkv": bf(np.random.standard_normal((HID, NQ + NK + NK)) / np.sqrt(HID) / s[:, None]),
            "q_norm_w": bf(1.0 + 0.1 * np.random.standard_normal(D)),
            "k_norm_w": bf(1.0 + 0.1 * np.random.standard_normal(D)),
            "cos": bf(np.cos(emb)), "sin": bf(np.sin(emb))}


def reference(hidden_states, w_qkv, q_norm_w, k_norm_w, cos, sin):
    qkv = mxq(f64(hidden_states), 1, "e4m3") @ mxq(f64(w_qkv), 0, "e4m3")
    q = qkv[:, :NQ].reshape(S, H, D)
    k = qkv[:, NQ:NQ + NK].reshape(S, KV, D)
    v = qkv[:, NQ + NK:].reshape(S, KV, D)
    q = rms_norm(q, f64(q_norm_w))
    k = rms_norm(k, f64(k_norm_w))
    q = apply_rope(q, f64(cos), f64(sin))
    k = apply_rope(k, f64(cos), f64(sin))
    return q, k, v

@@ -1,0 +1,285 @@
+from contextlib import ExitStack
+
+import concourse.mybir as mybir
+from concourse.masks import make_identity
+
+F32 = mybir.dt.float32
+BF16 = mybir.dt.bfloat16
+U32 = mybir.dt.uint32
+U8 = mybir.dt.uint8
+FP8X4 = mybir.dt.float8_e4m3fn_x4
+ACT = mybir.ActivationFunctionType
+ALU = mybir.AluOpType
+
+P = 128
+ROWS = 1024
+HID = 1024
+HEAD = 256
+HALF = HEAD // 2
+Q_COLS = 2048
+K_COLS = 1024
+V_COLS = 1024
+EPS = 1e-6
+
+PACK = 4
+K_PASS = P * PACK
+PASSES = HID // K_PASS
+ROW_TILES = ROWS // P
+BANK = 512
+CHUNK = 2 * BANK
+CHUNKS = (Q_COLS + K_COLS + V_COLS) // CHUNK
+CHUNK_HEADS = CHUNK // HEAD
+X_PIECES = 4
+PIECE_TILES = ROW_TILES // X_PIECES
+PIECE_ROWS = PIECE_TILES * P
+
+FLOPS = 2 * ROWS * HID * (Q_COLS + K_COLS + V_COLS)
+
+
+def tile_gemmaattention_pa_kernel(
+    tc, hidden_states, w_qkv, q_norm_w, k_norm_w, cos, sin, out_0, out_1, out_2
+):
+    nc = tc.nc
+
+    x_rows = hidden_states.rearrange("(p m) k -> p m k", m=ROW_TILES)
+    cos_rows = cos.rearrange("(p m) d -> p m d", m=ROW_TILES)
+    sin_rows = sin.rearrange("(p m) d -> p m d", m=ROW_TILES)
+    q_out = out_0.rearrange("(p m) h d -> m p (h d)", m=ROW_TILES)
+    k_out = out_1.rearrange("(p m) h d -> m p (h d)", m=ROW_TILES)
+    v_out = out_2.rearrange("(p m) h d -> m p (h d)", m=ROW_TILES)
+    chunk_out = [(q_out, 0), (q_out, CHUNK), (k_out, 0), (v_out, 0)]
+    VALUES = CHUNKS - 1
+
+    with ExitStack() as stack:
+        stack.enter_context(tc.manual_schedule())
+        keep = stack.enter_context(tc.tile_pool(name="keep", bufs=1))
+        w_raw_pool = stack.enter_context(tc.tile_pool(name="w_raw", bufs=6))
+        w_grouped_pool = stack.enter_context(tc.tile_pool(name="w_grouped", bufs=4))
+        x_grouped_pool = stack.enter_context(tc.tile_pool(name="x_grouped", bufs=2))
+        products_pool = stack.enter_context(tc.tile_pool(name="products", bufs=3))
+        result_pool = stack.enter_context(tc.tile_pool(name="result", bufs=4))
+        squares_pool = stack.enter_context(tc.tile_pool(name="squares", bufs=4))
+        stats_pool = stack.enter_context(tc.tile_pool(name="stats", bufs=6))
+        psum = stack.enter_context(tc.psum_pool(name="psum", bufs=8))
+
+        identity = keep.tile([P, P], F32)
+        eps = keep.tile([P, 1], F32)
+        warm = keep.tile([P, 1], F32)
+        x_raw = keep.tile([P, ROW_TILES * HID], BF16)
+        x_codes = keep.tile([P, X_PIECES, PASSES * PIECE_ROWS], U32, align_bytes=64)
+        x_scales = keep.tile([P, X_PIECES, PASSES * PIECE_ROWS], U8, align_bytes=64)
+        w_codes = keep.tile([P, PASSES, CHUNKS * CHUNK], U32, align_bytes=64)
+        w_scales = keep.tile([P, PASSES, CHUNKS * CHUNK], U8, align_bytes=64)
+        cos_raw = keep.tile([P, ROW_TILES, HEAD], BF16)
+        sin_raw = keep.tile([P, ROW_TILES, HEAD], BF16)
+        q_weight = keep.tile([P, HEAD], BF16)
+        k_weight = keep.tile([P, HEAD], BF16)
+        q_gain = keep.tile([P, 2, HEAD], F32)
+        k_gain = keep.tile([P, 2, HEAD], F32)
+        q_table = keep.tile([P, 2, ROW_TILES, HEAD], F32)
+        k_table = keep.tile([P, 2, ROW_TILES, HEAD], F32)
+
+        def load_x_piece(i):
+            cols = slice(i * PIECE_TILES * HID, (i + 1) * PIECE_TILES * HID)
+            nc.sync.dma_start(
+                out=x_raw[:, cols].rearrange("p (m k) -> p m k", m=PIECE_TILES),
+                in_=x_rows[:, i * PIECE_TILES : (i + 1) * PIECE_TILES, :],
+            )
+
+        def load_w(c, g):
+            raw = w_raw_pool.tile([P, PACK, CHUNK], BF16, tag="w_raw", name="w_raw_%d_%d" % (c, g))
+            nc.sync.dma_start(
+                out=raw[:],
+                in_=w_qkv[g * K_PASS : (g + 1) * K_PASS, c * CHUNK : (c + 1) * CHUNK].rearrange(
+                    "(p t) n -> p t n", t=PACK
+                ),
+            )
+            return raw
+
+        def quantise_x_piece(i):
+            x_words = x_raw[:].bitcast(F32)
+            words_per_row = HID // 2
+            words_per_pass = K_PASS // 2
+            grouped = x_grouped_pool.tile([P, PASSES * PIECE_ROWS * PACK], BF16, align_bytes=64, tag="x_grouped")
+            grouped_words = grouped[:].bitcast(F32).rearrange("p (g s u) -> p g s u", g=PASSES, u=2)
+            for local in range(PIECE_TILES):
+                m = i * PIECE_TILES + local
+                turned = psum.tile([P, BANK], F32, tag="bank", name="turned_%d" % m)
+                turned_gus = turned[:].rearrange("p (g u s) -> p g u s", g=PASSES, u=2)
+                for g in range(PASSES):
+                    for u in range(2):
+                        first = m * words_per_row + g * words_per_pass
+                        nc.tensor.transpose(
+                            turned_gus[:, g, u, :],
+                            x_words[:, first + u : first + words_per_pass : 2],
+                            identity[:],
+                        )
+                nc.scalar.copy(
+                    out=grouped_words[:, :, local * P : (local + 1) * P, :],
+                    in_=turned_gus.rearrange("p g u s -> p g s u"),
+                )
+            nc.vector.quantize_mx(
+                out=x_codes[:, i, :].bitcast(FP8X4), scales=x_scales[:, i, :], in_=grouped[:]
+            )
+
+        def regroup_w(engine_copy, raw, h):
+            grouped = w_grouped_pool.tile([P, BANK, PACK], BF16, align_bytes=64, tag="w_grouped")
+            engine_copy(
+                out=grouped[:].rearrange("p (n i) t -> p n t i", i=4),
+                in_=raw[:, :, h * BANK : (h + 1) * BANK].rearrange("p t (n i) -> p n t i", i=4),
+            )
+            return grouped
+
+        def quantise_w(grouped, c, g, h):
+            cols = slice(c * CHUNK + h * BANK, c * CHUNK + (h + 1) * BANK)
+            nc.vector.quantize_mx(
+                out=w_codes[:, g, cols].bitcast(FP8X4),
+                scales=w_scales[:, g, cols],
+                in_=grouped[:].rearrange("p n t -> p (n t)"),
+            )
+
+        def make_gain(gain, weight):
+            nc.vector.tensor_scalar_add(out=gain[:, 0, :], in0=weight[:], scalar1=1.0)
+            nc.vector.tensor_scalar_add(out=gain[:, 1, 0:HALF], in0=weight[:, 0:HALF], scalar1=1.0)
+            nc.vector.tensor_scalar(
+                out=gain[:, 1, HALF:HEAD], in0=weight[:, HALF:HEAD],
+                scalar1=-1.0, scalar2=-1.0, op0=ALU.mult, op1=ALU.add,
+            )
+
+        def make_table(engine, table, gain):
+            def over_tiles(row):
+                return row.unsqueeze(1).to_broadcast([P, ROW_TILES, row.shape[1]])
+
+            engine.tensor_tensor(
+                out=table[:, 0, :, :], in0=cos_raw[:], in1=over_tiles(gain[:, 0, :]), op=ALU.mult
+            )
+            engine.tensor_tensor(
+                out=table[:, 1, :, 0:HALF], in0=sin_raw[:, :, HALF:HEAD],
+                in1=over_tiles(gain[:, 1, 0:HALF]), op=ALU.mult,
+            )
+            engine.tensor_tensor(
+                out=table[:, 1, :, HALF:HEAD], in0=sin_raw[:, :, 0:HALF],
+                in1=over_tiles(gain[:, 1, HALF:HEAD]), op=ALU.mult,
+            )
+
+        def multiply(c, m):
+            banks = [psum.tile([P, BANK], F32, tag="bank", name="acc_%d_%d_%d" % (c, m, h)) for h in range(2)]
+            piece, local = divmod(m, PIECE_TILES)
+            for g in range(PASSES):
+                rows = slice(g * PIECE_ROWS + local * P, g * PIECE_ROWS + (local + 1) * P)
+                for h in range(2):
+                    cols = slice(c * CHUNK + h * BANK, c * CHUNK + (h + 1) * BANK)
+                    nc.tensor.matmul_mx(
+                        out=banks[h][:],
+                        lhsT=x_codes[:, piece, rows].bitcast(FP8X4),
+                        lhsT_scale=x_scales[:, piece, rows],
+                        rhs=w_codes[:, g, cols].bitcast(FP8X4),
+                        rhs_scale=w_scales[:, g, cols],
+                        start=(g == 0),
+                        stop=(g == PASSES - 1),
+                    )
+            return banks
+
+        def head_in_banks(banks, j):
+            heads_per_bank = BANK // HEAD
+            first = (j % heads_per_bank) * HEAD
+            return banks[j // heads_per_bank][:, first : first + HEAD]
+
+        def root_mean_square(banks):
+            sums = stats_pool.tile([P, CHUNK_HEADS], F32, tag="sums")
+            for j in range(CHUNK_HEADS):
+                squares = squares_pool.tile([P, HEAD], BF16, tag="squares")
+                nc.scalar.activation(
+                    out=squares[:], in_=head_in_banks(banks, j), func=ACT.Square,
+                    accum_out=sums[:, j : j + 1],
+                )
+            rms = stats_pool.tile([P, CHUNK_HEADS], F32, tag="rms")
+            nc.scalar.activation(out=rms[:], in_=sums[:], func=ACT.Sqrt, scale=1.0 / HEAD, bias=eps[:, 0:1])
+            return rms
+
+        def norm_and_rope(banks, rms, table, m):
+            inverse = stats_pool.tile([P, CHUNK_HEADS], F32, tag="inverse")
+            nc.vector.reciprocal(out=inverse[:], in_=rms[:])
+            products = products_pool.tile([P, CHUNK_HEADS, 2, HEAD], F32, tag="products")
+            for j in range(CHUNK_HEADS):
+                nc.vector.scalar_tensor_tensor(
+                    out=products[:, j, :, :],
+                    in0=head_in_banks(banks, j).unsqueeze(1).to_broadcast([P, 2, HEAD]),
+                    scalar=inverse[:, j : j + 1],
+                    in1=table[:, :, m, :],
+                    op0=ALU.mult,
+                    op1=ALU.mult,
+                )
+            result = result_pool.tile([P, CHUNK_HEADS, HEAD], F32, tag="result")
+            nc.gpsimd.tensor_tensor(
+                out=result[:, :, 0:HALF], in0=products[:, :, 0, 0:HALF],
+                in1=products[:, :, 1, HALF:HEAD], op=ALU.add,
+            )
+            nc.gpsimd.tensor_tensor(
+                out=result[:, :, HALF:HEAD], in0=products[:, :, 0, HALF:HEAD],
+                in1=products[:, :, 1, 0:HALF], op=ALU.add,
+            )
+            return result
+
+        def copy_values(banks):
+            result = result_pool.tile([P, CHUNK_HEADS, HEAD], F32, tag="result")
+            flat = result[:].rearrange("p j d -> p (j d)")
+            nc.scalar.copy(out=flat[:, 0:BANK], in_=banks[0][:])
+            nc.vector.tensor_copy(out=flat[:, BANK:CHUNK], in_=banks[1][:])
+            return result
+
+        nc.scalar.dma_start(out=q_weight[:], in_=q_norm_w.partition_broadcast(P))
+        nc.scalar.dma_start(out=k_weight[:], in_=k_norm_w.partition_broadcast(P))
+        w_raw = {}
+        load_x_piece(0)
+        nc.sync.dma_start(out=cos_raw[:], in_=cos_rows)
+        nc.sync.dma_start(out=sin_raw[:], in_=sin_rows)
+        for g in range(PASSES):
+            w_raw[(0, g)] = load_w(0, g)
+        for i in range(1, X_PIECES):
+            load_x_piece(i)
+        for c in (1, 2):
+            for g in range(PASSES):
+                w_raw[(c, g)] = load_w(c, g)
+
+        make_identity(nc, identity[:])
+        nc.vector.memset(eps[:], EPS)
+        nc.scalar.activation(out=warm[:], in_=eps[:], func=ACT.Sqrt)
+        make_gain(q_gain, q_weight)
+        make_gain(k_gain, k_weight)
+        make_table(nc.gpsimd, k_table, k_gain)
+
+        quantise_x_piece(0)
+        make_table(nc.vector, q_table, q_gain)
+        first_grouped = {}
+        for g in range(PASSES):
+            first_grouped[(g, 0)] = regroup_w(nc.vector.tensor_copy, w_raw[(0, g)], 0)
+            first_grouped[(g, 1)] = regroup_w(nc.scalar.copy, w_raw[(0, g)], 1)
+        for g in range(PASSES):
+            for h in range(2):
+                quantise_w(first_grouped[(g, h)], 0, g, h)
+        for g in range(PASSES):
+            w_raw[(CHUNKS - 1, g)] = load_w(CHUNKS - 1, g)
+        for i in range(1, X_PIECES):
+            quantise_x_piece(i)
+
+        for c in range(CHUNKS):
+            waiting = None
+            for m in range(ROW_TILES):
+                banks = multiply(c, m)
+                if c != VALUES:
+                    rms = root_mean_square(banks)
+                if waiting is not None:
+                    quantise_w(waiting[0], c + 1, waiting[1], waiting[2])
+                    waiting = None
+                if c + 1 < CHUNKS and m < PASSES * 2:
+                    g, h = divmod(m, 2)
+                    waiting = (regroup_w(nc.scalar.copy, w_raw[(c + 1, g)], h), g, h)
+                if c != VALUES:
+                    result = norm_and_rope(banks, rms, q_table if c < 2 else k_table, m)
+                else:
+                    result = copy_values(banks)
+                view, first = chunk_out[c]
+                nc.sync.dma_start(
+                    out=view[m, :, first : first + CHUNK], in_=result[:].rearrange("p j d -> p (j d)")
+                )

@@ -140,27 +140,25 @@ def tile_gemmaattention_pa_kernel(
 
         def make_gain(gain, weight):
             nc.vector.tensor_scalar_add(out=gain[:, 0, :], in0=weight[:], scalar1=1.0)
-            nc.vector.tensor_scalar_add(out=gain[:, 1, 0:HALF], in0=weight[:, 0:HALF], scalar1=1.0)
             nc.vector.tensor_scalar(
-                out=gain[:, 1, HALF:HEAD], in0=weight[:, HALF:HEAD],
-                scalar1=-1.0, scalar2=-1.0, op0=ALU.mult, op1=ALU.add,
+                out=gain[:, 1, :], in0=weight[:], scalar1=-1.0, scalar2=-1.0, op0=ALU.mult, op1=ALU.add
             )
 
         def make_table(engine, table, gain):
             def over_tiles(row):
                 return row.unsqueeze(1).to_broadcast([P, ROW_TILES, row.shape[1]])
 
-            engine.tensor_tensor(
-                out=table[:, 0, :, :], in0=cos_raw[:], in1=over_tiles(gain[:, 0, :]), op=ALU.mult
-            )
-            engine.tensor_tensor(
-                out=table[:, 1, :, 0:HALF], in0=sin_raw[:, :, HALF:HEAD],
-                in1=over_tiles(gain[:, 1, 0:HALF]), op=ALU.mult,
-            )
-            engine.tensor_tensor(
-                out=table[:, 1, :, HALF:HEAD], in0=sin_raw[:, :, 0:HALF],
-                in1=over_tiles(gain[:, 1, HALF:HEAD]), op=ALU.mult,
-            )
+            low, high = slice(0, HALF), slice(HALF, HEAD)
+            for r, x_half, angles, angle_half, sign in (
+                (0, low, cos_raw, low, 0),
+                (0, high, sin_raw, low, 1),
+                (1, low, sin_raw, high, 0),
+                (1, high, cos_raw, high, 0),
+            ):
+                engine.tensor_tensor(
+                    out=table[:, r, :, x_half], in0=angles[:, :, angle_half],
+                    in1=over_tiles(gain[:, sign, x_half]), op=ALU.mult,
+                )
 
         def multiply(c, m):
             banks = [psum.tile([P, BANK], F32, tag="bank", name="acc_%d_%d_%d" % (c, m, h)) for h in range(2)]
@@ -185,7 +183,7 @@ def tile_gemmaattention_pa_kernel(
             first = (j % heads_per_bank) * HEAD
             return banks[j // heads_per_bank][:, first : first + HEAD]
 
-        def root_mean_square(banks):
+        def sum_squares(banks):
             sums = stats_pool.tile([P, CHUNK_HEADS], F32, tag="sums")
             for j in range(CHUNK_HEADS):
                 squares = squares_pool.tile([P, HEAD], BF16, tag="squares")
@@ -193,13 +191,16 @@ def tile_gemmaattention_pa_kernel(
                     out=squares[:], in_=head_in_banks(banks, j), func=ACT.Square,
                     accum_out=sums[:, j : j + 1],
                 )
-            rms = stats_pool.tile([P, CHUNK_HEADS], F32, tag="rms")
-            nc.scalar.activation(out=rms[:], in_=sums[:], func=ACT.Sqrt, scale=1.0 / HEAD, bias=eps[:, 0:1])
-            return rms
+            return sums
 
-        def norm_and_rope(banks, rms, table, m):
+        def inverse_rms(sums):
             inverse = stats_pool.tile([P, CHUNK_HEADS], F32, tag="inverse")
-            nc.vector.reciprocal(out=inverse[:], in_=rms[:])
+            nc.scalar.activation(
+                out=inverse[:], in_=sums[:], func=ACT.Abs_reciprocal_sqrt, scale=1.0 / HEAD, bias=eps[:, 0:1]
+            )
+            return inverse
+
+        def norm_and_rope(banks, inverse, table, m):
             products = products_pool.tile([P, CHUNK_HEADS, 2, HEAD], F32, tag="products")
             for j in range(CHUNK_HEADS):
                 nc.vector.scalar_tensor_tensor(
@@ -211,13 +212,10 @@ def tile_gemmaattention_pa_kernel(
                     op1=ALU.mult,
                 )
             result = result_pool.tile([P, CHUNK_HEADS, HEAD], F32, tag="result")
+            terms = products[:].rearrange("p j r (x i) -> p (j r) x i", x=2)
             nc.gpsimd.tensor_tensor(
-                out=result[:, :, 0:HALF], in0=products[:, :, 0, 0:HALF],
-                in1=products[:, :, 1, HALF:HEAD], op=ALU.add,
-            )
-            nc.gpsimd.tensor_tensor(
-                out=result[:, :, HALF:HEAD], in0=products[:, :, 0, HALF:HEAD],
-                in1=products[:, :, 1, 0:HALF], op=ALU.add,
+                out=result[:].rearrange("p j (r i) -> p (j r) i", r=2),
+                in0=terms[:, :, 0, :], in1=terms[:, :, 1, :], op=ALU.add,
             )
             return result
 
@@ -231,9 +229,9 @@ def tile_gemmaattention_pa_kernel(
         nc.scalar.dma_start(out=q_weight[:], in_=q_norm_w.partition_broadcast(P))
         nc.scalar.dma_start(out=k_weight[:], in_=k_norm_w.partition_broadcast(P))
         w_raw = {}
-        load_x_piece(0)
         nc.sync.dma_start(out=cos_raw[:], in_=cos_rows)
         nc.sync.dma_start(out=sin_raw[:], in_=sin_rows)
+        load_x_piece(0)
         for g in range(PASSES):
             w_raw[(0, g)] = load_w(0, g)
         for i in range(1, X_PIECES):
@@ -244,13 +242,13 @@ def tile_gemmaattention_pa_kernel(
 
         make_identity(nc, identity[:])
         nc.vector.memset(eps[:], EPS)
-        nc.scalar.activation(out=warm[:], in_=eps[:], func=ACT.Sqrt)
+        nc.scalar.activation(out=warm[:], in_=eps[:], func=ACT.Abs_reciprocal_sqrt)
         make_gain(q_gain, q_weight)
         make_gain(k_gain, k_weight)
         make_table(nc.gpsimd, k_table, k_gain)
+        make_table(nc.vector, q_table, q_gain)
 
         quantise_x_piece(0)
-        make_table(nc.vector, q_table, q_gain)
         first_grouped = {}
         for g in range(PASSES):
             first_grouped[(g, 0)] = regroup_w(nc.vector.tensor_copy, w_raw[(0, g)], 0)
@@ -268,15 +266,15 @@ def tile_gemmaattention_pa_kernel(
             for m in range(ROW_TILES):
                 banks = multiply(c, m)
                 if c != VALUES:
-                    rms = root_mean_square(banks)
+                    inverse = inverse_rms(sum_squares(banks))
                 if waiting is not None:
                     quantise_w(waiting[0], c + 1, waiting[1], waiting[2])
                     waiting = None
-                if c + 1 < CHUNKS and m < PASSES * 2:
-                    g, h = divmod(m, 2)
+                if c + 1 < CHUNKS and m % 2 == 0:
+                    g, h = divmod(m // 2, 2)
                     waiting = (regroup_w(nc.scalar.copy, w_raw[(c + 1, g)], h), g, h)
                 if c != VALUES:
-                    result = norm_and_rope(banks, rms, q_table if c < 2 else k_table, m)
+                    result = norm_and_rope(banks, inverse, q_table if c < 2 else k_table, m)
                 else:
                     result = copy_values(banks)
                 view, first = chunk_out[c]

@@ -55,7 +55,6 @@ def tile_gemmaattention_pa_kernel(
         keep = stack.enter_context(tc.tile_pool(name="keep", bufs=1))
         w_raw_pool = stack.enter_context(tc.tile_pool(name="w_raw", bufs=6))
         w_grouped_pool = stack.enter_context(tc.tile_pool(name="w_grouped", bufs=4))
-        x_grouped_pool = stack.enter_context(tc.tile_pool(name="x_grouped", bufs=2))
         products_pool = stack.enter_context(tc.tile_pool(name="products", bufs=3))
         result_pool = stack.enter_context(tc.tile_pool(name="result", bufs=4))
         squares_pool = stack.enter_context(tc.tile_pool(name="squares", bufs=4))
@@ -65,13 +64,10 @@ def tile_gemmaattention_pa_kernel(
         identity = keep.tile([P, P], F32)
         eps = keep.tile([P, 1], F32)
         warm = keep.tile([P, 1], F32)
-        x_raw = keep.tile([P, ROW_TILES * HID], BF16)
         x_codes = keep.tile([P, X_PIECES, PASSES * PIECE_ROWS], U32, align_bytes=64)
         x_scales = keep.tile([P, X_PIECES, PASSES * PIECE_ROWS], U8, align_bytes=64)
         w_codes = keep.tile([P, PASSES, CHUNKS * CHUNK], U32, align_bytes=64)
         w_scales = keep.tile([P, PASSES, CHUNKS * CHUNK], U8, align_bytes=64)
-        cos_raw = keep.tile([P, ROW_TILES, HEAD], BF16)
-        sin_raw = keep.tile([P, ROW_TILES, HEAD], BF16)
         q_weight = keep.tile([P, HEAD], BF16)
         k_weight = keep.tile([P, HEAD], BF16)
         q_gain = keep.tile([P, 2, HEAD], F32)
@@ -122,13 +118,14 @@ def tile_gemmaattention_pa_kernel(
                 out=x_codes[:, i, :].bitcast(FP8X4), scales=x_scales[:, i, :], in_=grouped[:]
             )
 
-        def regroup_w(engine_copy, raw, h):
-            grouped = w_grouped_pool.tile([P, BANK, PACK], BF16, align_bytes=64, tag="w_grouped")
+        def new_grouped():
+            return w_grouped_pool.tile([P, BANK, PACK], BF16, align_bytes=64, tag="w_grouped", name="w_grouped")
+
+        def regroup_w(engine_copy, grouped, raw, h, first, count):
             engine_copy(
-                out=grouped[:].rearrange("p (n i) t -> p n t i", i=4),
-                in_=raw[:, :, h * BANK : (h + 1) * BANK].rearrange("p t (n i) -> p n t i", i=4),
+                out=grouped[:, first : first + count, :].rearrange("p (n i) t -> p n t i", i=4),
+                in_=raw[:, :, h * BANK + first : h * BANK + first + count].rearrange("p t (n i) -> p n t i", i=4),
             )
-            return grouped
 
         def quantise_w(grouped, c, g, h):
             cols = slice(c * CHUNK + h * BANK, c * CHUNK + (h + 1) * BANK)
@@ -220,64 +217,78 @@ def tile_gemmaattention_pa_kernel(
             return result
 
         def copy_values(banks):
-            result = result_pool.tile([P, CHUNK_HEADS, HEAD], F32, tag="result")
-            flat = result[:].rearrange("p j d -> p (j d)")
-            nc.scalar.copy(out=flat[:, 0:BANK], in_=banks[0][:])
-            nc.vector.tensor_copy(out=flat[:, BANK:CHUNK], in_=banks[1][:])
+            result = values_pool.tile([P, CHUNK], F32, tag="values")
+            nc.scalar.copy(out=result[:, 0:BANK], in_=banks[0][:])
+            nc.scalar.copy(out=result[:, BANK:CHUNK], in_=banks[1][:])
             return result
 
-        nc.scalar.dma_start(out=q_weight[:], in_=q_norm_w.partition_broadcast(P))
-        nc.scalar.dma_start(out=k_weight[:], in_=k_norm_w.partition_broadcast(P))
-        w_raw = {}
-        nc.sync.dma_start(out=cos_raw[:], in_=cos_rows)
-        nc.sync.dma_start(out=sin_raw[:], in_=sin_rows)
-        load_x_piece(0)
-        for g in range(PASSES):
-            w_raw[(0, g)] = load_w(0, g)
-        for i in range(1, X_PIECES):
-            load_x_piece(i)
-        for c in (1, 2):
+        with tc.tile_pool(name="start", bufs=1) as start, tc.tile_pool(name="x_grouped", bufs=2) as x_grouped_pool:
+            x_raw = start.tile([P, ROW_TILES * HID], BF16)
+            cos_raw = start.tile([P, ROW_TILES, HEAD], BF16)
+            sin_raw = start.tile([P, ROW_TILES, HEAD], BF16)
+
+            nc.scalar.dma_start(out=q_weight[:], in_=q_norm_w.partition_broadcast(P))
+            nc.scalar.dma_start(out=k_weight[:], in_=k_norm_w.partition_broadcast(P))
+            w_raw = {}
+            nc.sync.dma_start(out=cos_raw[:], in_=cos_rows)
+            nc.sync.dma_start(out=sin_raw[:], in_=sin_rows)
+            load_x_piece(0)
             for g in range(PASSES):
-                w_raw[(c, g)] = load_w(c, g)
+                w_raw[(0, g)] = load_w(0, g)
+            for i in range(1, X_PIECES):
+                load_x_piece(i)
+            for c in (1, 2):
+                for g in range(PASSES):
+                    w_raw[(c, g)] = load_w(c, g)
 
-        make_identity(nc, identity[:])
-        nc.vector.memset(eps[:], EPS)
-        nc.scalar.activation(out=warm[:], in_=eps[:], func=ACT.Abs_reciprocal_sqrt)
-        make_gain(q_gain, q_weight)
-        make_gain(k_gain, k_weight)
-        make_table(nc.gpsimd, k_table, k_gain)
-        make_table(nc.vector, q_table, q_gain)
+            make_identity(nc, identity[:])
+            nc.vector.memset(eps[:], EPS)
+            nc.scalar.activation(out=warm[:], in_=eps[:], func=ACT.Abs_reciprocal_sqrt)
+            make_gain(q_gain, q_weight)
+            make_gain(k_gain, k_weight)
+            make_table(nc.gpsimd, k_table, k_gain)
+            make_table(nc.vector, q_table, q_gain)
 
-        quantise_x_piece(0)
-        first_grouped = {}
-        for g in range(PASSES):
-            first_grouped[(g, 0)] = regroup_w(nc.vector.tensor_copy, w_raw[(0, g)], 0)
-            first_grouped[(g, 1)] = regroup_w(nc.scalar.copy, w_raw[(0, g)], 1)
-        for g in range(PASSES):
-            for h in range(2):
-                quantise_w(first_grouped[(g, h)], 0, g, h)
-        for g in range(PASSES):
-            w_raw[(CHUNKS - 1, g)] = load_w(CHUNKS - 1, g)
-        for i in range(1, X_PIECES):
-            quantise_x_piece(i)
+            quantise_x_piece(0)
+            first_grouped = {}
+            for g in range(PASSES):
+                for h, engine_copy in ((0, nc.vector.tensor_copy), (1, nc.scalar.copy)):
+                    first_grouped[(g, h)] = new_grouped()
+                    regroup_w(engine_copy, first_grouped[(g, h)], w_raw[(0, g)], h, 0, BANK)
+            for g in range(PASSES):
+                for h in range(2):
+                    quantise_w(first_grouped[(g, h)], 0, g, h)
+            for g in range(PASSES):
+                w_raw[(CHUNKS - 1, g)] = load_w(CHUNKS - 1, g)
+            for i in range(1, X_PIECES):
+                quantise_x_piece(i)
 
+            operands = [(c, g, h) for c in range(1, CHUNKS) for g in range(PASSES) for h in range(2)]
+            grouped = new_grouped()
+            regroup_w(nc.vector.tensor_copy, grouped, w_raw[(operands[0][0], operands[0][1])], operands[0][2], 0, BANK)
+        values_pool = stack.enter_context(tc.tile_pool(name="values", bufs=4))
+
+        HALF_BANK = BANK // 2
         for c in range(CHUNKS):
-            waiting = None
             for m in range(ROW_TILES):
                 banks = multiply(c, m)
-                if c != VALUES:
-                    inverse = inverse_rms(sum_squares(banks))
-                if waiting is not None:
-                    quantise_w(waiting[0], c + 1, waiting[1], waiting[2])
-                    waiting = None
-                if c + 1 < CHUNKS and m % 2 == 0:
-                    g, h = divmod(m // 2, 2)
-                    waiting = (regroup_w(nc.scalar.copy, w_raw[(c + 1, g)], h), g, h)
-                if c != VALUES:
-                    result = norm_and_rope(banks, inverse, q_table if c < 2 else k_table, m)
-                else:
-                    result = copy_values(banks)
                 view, first = chunk_out[c]
-                nc.sync.dma_start(
-                    out=view[m, :, first : first + CHUNK], in_=result[:].rearrange("p j d -> p (j d)")
-                )
+                if c == VALUES:
+                    nc.scalar.dma_start(out=view[m, :, first : first + CHUNK], in_=copy_values(banks)[:])
+                else:
+                    sums = sum_squares(banks)
+                    number, part = divmod(c * ROW_TILES + m + 2, 2)
+                    if part == 0:
+                        done_c, done_g, done_h = operands[number - 1]
+                        quantise_w(grouped, done_c, done_g, done_h)
+                    if number < len(operands):
+                        next_c, next_g, next_h = operands[number]
+                        if part == 0:
+                            grouped = new_grouped()
+                        regroup_w(
+                            nc.scalar.copy, grouped, w_raw[(next_c, next_g)], next_h, part * HALF_BANK, HALF_BANK
+                        )
+                    result = norm_and_rope(banks, inverse_rms(sums), q_table if c < 2 else k_table, m)
+                    nc.sync.dma_start(
+                        out=view[m, :, first : first + CHUNK], in_=result[:].rearrange("p j d -> p (j d)")
+                    )

@@ -68,8 +68,6 @@ def tile_gemmaattention_pa_kernel(
         x_scales = keep.tile([P, X_PIECES, PASSES * PIECE_ROWS], U8, align_bytes=64)
         w_codes = keep.tile([P, PASSES, CHUNKS * CHUNK], U32, align_bytes=64)
         w_scales = keep.tile([P, PASSES, CHUNKS * CHUNK], U8, align_bytes=64)
-        q_weight = keep.tile([P, HEAD], BF16)
-        k_weight = keep.tile([P, HEAD], BF16)
         q_gain = keep.tile([P, 2, HEAD], F32)
         k_gain = keep.tile([P, 2, HEAD], F32)
         q_table = keep.tile([P, 2, ROW_TILES, HEAD], F32)
@@ -136,9 +134,9 @@ def tile_gemmaattention_pa_kernel(
             )
 
         def make_gain(gain, weight):
-            nc.vector.tensor_scalar_add(out=gain[:, 0, :], in0=weight[:], scalar1=1.0)
+            nc.vector.tensor_scalar_add(out=gain[:, 0, :], in0=weight, scalar1=1.0)
             nc.vector.tensor_scalar(
-                out=gain[:, 1, :], in0=weight[:], scalar1=-1.0, scalar2=-1.0, op0=ALU.mult, op1=ALU.add
+                out=gain[:, 1, :], in0=weight, scalar1=-1.0, scalar2=-1.0, op0=ALU.mult, op1=ALU.add
             )
 
         def make_table(engine, table, gain):
@@ -226,9 +224,12 @@ def tile_gemmaattention_pa_kernel(
             x_raw = start.tile([P, ROW_TILES * HID], BF16)
             cos_raw = start.tile([P, ROW_TILES, HEAD], BF16)
             sin_raw = start.tile([P, ROW_TILES, HEAD], BF16)
+            ones = start.tile([P, P], BF16)
+            weight_rows = start.tile([P, 2 * HEAD], BF16)
 
-            nc.scalar.dma_start(out=q_weight[:], in_=q_norm_w.partition_broadcast(P))
-            nc.scalar.dma_start(out=k_weight[:], in_=k_norm_w.partition_broadcast(P))
+            nc.vector.memset(weight_rows[:], 0.0)
+            nc.scalar.dma_start(out=weight_rows[0:1, 0:HEAD], in_=q_norm_w.unsqueeze(0))
+            nc.scalar.dma_start(out=weight_rows[0:1, HEAD : 2 * HEAD], in_=k_norm_w.unsqueeze(0))
             w_raw = {}
             nc.sync.dma_start(out=cos_raw[:], in_=cos_rows)
             nc.sync.dma_start(out=sin_raw[:], in_=sin_rows)
@@ -244,8 +245,11 @@ def tile_gemmaattention_pa_kernel(
             make_identity(nc, identity[:])
             nc.vector.memset(eps[:], EPS)
             nc.scalar.activation(out=warm[:], in_=eps[:], func=ACT.Abs_reciprocal_sqrt)
-            make_gain(q_gain, q_weight)
-            make_gain(k_gain, k_weight)
+            nc.vector.memset(ones[:], 1.0)
+            spread = psum.tile([P, BANK], F32, tag="bank")
+            nc.tensor.matmul(out=spread[:], lhsT=ones[:], rhs=weight_rows[:], start=True, stop=True)
+            make_gain(q_gain, spread[:, 0:HEAD])
+            make_gain(k_gain, spread[:, HEAD : 2 * HEAD])
             make_table(nc.gpsimd, k_table, k_gain)
             make_table(nc.vector, q_table, q_gain)
 

@@ -68,8 +68,6 @@ def tile_gemmaattention_pa_kernel(
         x_scales = keep.tile([P, X_PIECES, PASSES * PIECE_ROWS], U8, align_bytes=64)
         w_codes = keep.tile([P, PASSES, CHUNKS * CHUNK], U32, align_bytes=64)
         w_scales = keep.tile([P, PASSES, CHUNKS * CHUNK], U8, align_bytes=64)
-        q_gain = keep.tile([P, 2, HEAD], F32)
-        k_gain = keep.tile([P, 2, HEAD], F32)
         q_table = keep.tile([P, 2, ROW_TILES, HEAD], F32)
         k_table = keep.tile([P, 2, ROW_TILES, HEAD], F32)
 
@@ -133,26 +131,22 @@ def tile_gemmaattention_pa_kernel(
                 in_=grouped[:].rearrange("p n t -> p (n t)"),
             )
 
-        def make_gain(gain, weight):
-            nc.vector.tensor_scalar_add(out=gain[:, 0, :], in0=weight, scalar1=1.0)
-            nc.vector.tensor_scalar(
-                out=gain[:, 1, :], in0=weight, scalar1=-1.0, scalar2=-1.0, op0=ALU.mult, op1=ALU.add
-            )
-
-        def make_table(engine, table, gain):
-            def over_tiles(row):
-                return row.unsqueeze(1).to_broadcast([P, ROW_TILES, row.shape[1]])
-
+        def make_table(table, first):
             low, high = slice(0, HALF), slice(HALF, HEAD)
-            for r, x_half, angles, angle_half, sign in (
-                (0, low, cos_raw, low, 0),
-                (0, high, sin_raw, low, 1),
-                (1, low, sin_raw, high, 0),
-                (1, high, cos_raw, high, 0),
+            for r, x_half, angles, angle_half, spread, one in (
+                (0, low, cos_raw, low, spread_plus, 1.0),
+                (0, high, sin_raw, low, spread_minus, -1.0),
+                (1, low, sin_raw, high, spread_plus, 1.0),
+                (1, high, cos_raw, high, spread_plus, 1.0),
             ):
-                engine.tensor_tensor(
-                    out=table[:, r, :, x_half], in0=angles[:, :, angle_half],
-                    in1=over_tiles(gain[:, sign, x_half]), op=ALU.mult,
+                weight = spread[:, first + x_half.start : first + x_half.stop]
+                nc.vector.scalar_tensor_tensor(
+                    out=table[:, r, :, x_half],
+                    in0=weight.unsqueeze(1).to_broadcast([P, ROW_TILES, HALF]),
+                    scalar=one,
+                    in1=angles[:, :, angle_half],
+                    op0=ALU.add,
+                    op1=ALU.mult,
                 )
 
         def multiply(c, m):
@@ -225,13 +219,14 @@ def tile_gemmaattention_pa_kernel(
             cos_raw = start.tile([P, ROW_TILES, HEAD], BF16)
             sin_raw = start.tile([P, ROW_TILES, HEAD], BF16)
             ones = start.tile([P, P], BF16)
+            minus_ones = start.tile([P, P], BF16)
             weight_rows = start.tile([P, 2 * HEAD], BF16)
 
             nc.vector.memset(weight_rows[:], 0.0)
-            nc.scalar.dma_start(out=weight_rows[0:1, 0:HEAD], in_=q_norm_w.unsqueeze(0))
-            nc.scalar.dma_start(out=weight_rows[0:1, HEAD : 2 * HEAD], in_=k_norm_w.unsqueeze(0))
             w_raw = {}
             nc.sync.dma_start(out=cos_raw[:], in_=cos_rows)
+            nc.sync.dma_start(out=weight_rows[0:1, 0:HEAD], in_=q_norm_w.unsqueeze(0))
+            nc.sync.dma_start(out=weight_rows[0:1, HEAD : 2 * HEAD], in_=k_norm_w.unsqueeze(0))
             nc.sync.dma_start(out=sin_raw[:], in_=sin_rows)
             load_x_piece(0)
             for g in range(PASSES):
@@ -246,12 +241,13 @@ def tile_gemmaattention_pa_kernel(
             nc.vector.memset(eps[:], EPS)
             nc.scalar.activation(out=warm[:], in_=eps[:], func=ACT.Abs_reciprocal_sqrt)
             nc.vector.memset(ones[:], 1.0)
-            spread = psum.tile([P, BANK], F32, tag="bank")
-            nc.tensor.matmul(out=spread[:], lhsT=ones[:], rhs=weight_rows[:], start=True, stop=True)
-            make_gain(q_gain, spread[:, 0:HEAD])
-            make_gain(k_gain, spread[:, HEAD : 2 * HEAD])
-            make_table(nc.gpsimd, k_table, k_gain)
-            make_table(nc.vector, q_table, q_gain)
+            nc.vector.memset(minus_ones[:], -1.0)
+            spread_plus = psum.tile([P, BANK], F32, tag="bank")
+            spread_minus = psum.tile([P, BANK], F32, tag="bank")
+            nc.tensor.matmul(out=spread_plus[:], lhsT=ones[:], rhs=weight_rows[:], start=True, stop=True)
+            nc.tensor.matmul(out=spread_minus[:], lhsT=minus_ones[:], rhs=weight_rows[:], start=True, stop=True)
+            make_table(q_table, 0)
+            make_table(k_table, HEAD)
 
             quantise_x_piece(0)
             first_grouped = {}

@@ -26,6 +26,7 @@ K_PASS = P * PACK
 PASSES = HID // K_PASS
 ROW_TILES = ROWS // P
 BANK = 512
+HALF_BANK = BANK // 2
 CHUNK = 2 * BANK
 CHUNKS = (Q_COLS + K_COLS + V_COLS) // CHUNK
 CHUNK_HEADS = CHUNK // HEAD
@@ -59,9 +60,11 @@ def tile_gemmaattention_pa_kernel(
         result_pool = stack.enter_context(tc.tile_pool(name="result", bufs=4))
         squares_pool = stack.enter_context(tc.tile_pool(name="squares", bufs=4))
         stats_pool = stack.enter_context(tc.tile_pool(name="stats", bufs=6))
-        psum = stack.enter_context(tc.psum_pool(name="psum", bufs=8))
+        acc_pool = stack.enter_context(tc.psum_pool(name="acc", bufs=6))
+        side_pool = stack.enter_context(tc.psum_pool(name="side", bufs=2))
 
         identity = keep.tile([P, P], F32)
+        identity_bf = keep.tile([P, P], BF16)
         eps = keep.tile([P, 1], F32)
         warm = keep.tile([P, 1], F32)
         x_codes = keep.tile([P, X_PIECES, PASSES * PIECE_ROWS], U32, align_bytes=64)
@@ -96,7 +99,7 @@ def tile_gemmaattention_pa_kernel(
             grouped_words = grouped[:].bitcast(F32).rearrange("p (g s u) -> p g s u", g=PASSES, u=2)
             for local in range(PIECE_TILES):
                 m = i * PIECE_TILES + local
-                turned = psum.tile([P, BANK], F32, tag="bank", name="turned_%d" % m)
+                turned = acc_pool.tile([P, BANK], F32, tag="acc", name="turned_%d" % m)
                 turned_gus = turned[:].rearrange("p (g u s) -> p g u s", g=PASSES, u=2)
                 for g in range(PASSES):
                     for u in range(2):
@@ -149,8 +152,21 @@ def tile_gemmaattention_pa_kernel(
                     op1=ALU.mult,
                 )
 
-        def multiply(c, m):
-            banks = [psum.tile([P, BANK], F32, tag="bank", name="acc_%d_%d_%d" % (c, m, h)) for h in range(2)]
+        def pass_through(raw, h, part):
+            bank = side_pool.tile([P, 2 * BANK], BF16, tag="side", name="through")
+            for q in range(2):
+                first = h * BANK + part * HALF_BANK + q * P
+                nc.tensor.matmul(
+                    out=bank[:, q * BANK : (q + 1) * BANK].rearrange("p (n t) -> p n t", t=PACK),
+                    lhsT=identity_bf[:],
+                    rhs=raw[:, :, first : first + P].rearrange("p t n -> p n t"),
+                    start=True,
+                    stop=True,
+                )
+            return bank
+
+        def multiply(c, m, pool, tag):
+            banks = [pool.tile([P, BANK], F32, tag=tag, name="acc_%d_%d_%d" % (c, m, h)) for h in range(2)]
             piece, local = divmod(m, PIECE_TILES)
             for g in range(PASSES):
                 rows = slice(g * PIECE_ROWS + local * P, g * PIECE_ROWS + (local + 1) * P)
@@ -238,12 +254,13 @@ def tile_gemmaattention_pa_kernel(
                     w_raw[(c, g)] = load_w(c, g)
 
             make_identity(nc, identity[:])
+            make_identity(nc, identity_bf[:])
             nc.vector.memset(eps[:], EPS)
             nc.scalar.activation(out=warm[:], in_=eps[:], func=ACT.Abs_reciprocal_sqrt)
             nc.vector.memset(ones[:], 1.0)
             nc.vector.memset(minus_ones[:], -1.0)
-            spread_plus = psum.tile([P, BANK], F32, tag="bank")
-            spread_minus = psum.tile([P, BANK], F32, tag="bank")
+            spread_plus = side_pool.tile([P, BANK], F32, tag="side")
+            spread_minus = side_pool.tile([P, BANK], F32, tag="side")
             nc.tensor.matmul(out=spread_plus[:], lhsT=ones[:], rhs=weight_rows[:], start=True, stop=True)
             nc.tensor.matmul(out=spread_minus[:], lhsT=minus_ones[:], rhs=weight_rows[:], start=True, stop=True)
             make_table(q_table, 0)
@@ -263,32 +280,51 @@ def tile_gemmaattention_pa_kernel(
             for i in range(1, X_PIECES):
                 quantise_x_piece(i)
 
-            operands = [(c, g, h) for c in range(1, CHUNKS) for g in range(PASSES) for h in range(2)]
-            grouped = new_grouped()
-            regroup_w(nc.vector.tensor_copy, grouped, w_raw[(operands[0][0], operands[0][1])], operands[0][2], 0, BANK)
         values_pool = stack.enter_context(tc.tile_pool(name="values", bufs=4))
 
-        HALF_BANK = BANK // 2
-        for c in range(CHUNKS):
-            for m in range(ROW_TILES):
-                banks = multiply(c, m)
-                view, first = chunk_out[c]
-                if c == VALUES:
-                    nc.scalar.dma_start(out=view[m, :, first : first + CHUNK], in_=copy_values(banks)[:])
-                else:
-                    sums = sum_squares(banks)
-                    number, part = divmod(c * ROW_TILES + m + 2, 2)
-                    if part == 0:
-                        done_c, done_g, done_h = operands[number - 1]
-                        quantise_w(grouped, done_c, done_g, done_h)
-                    if number < len(operands):
-                        next_c, next_g, next_h = operands[number]
-                        if part == 0:
-                            grouped = new_grouped()
-                        regroup_w(
-                            nc.scalar.copy, grouped, w_raw[(next_c, next_g)], next_h, part * HALF_BANK, HALF_BANK
-                        )
-                    result = norm_and_rope(banks, inverse_rms(sums), q_table if c < 2 else k_table, m)
-                    nc.sync.dma_start(
-                        out=view[m, :, first : first + CHUNK], in_=result[:].rearrange("p j d -> p (j d)")
+        operands = [(c, g, h) for c in range(1, CHUNKS) for g in range(PASSES) for h in range(2)]
+        steps = [(c, m) for c in range(VALUES) for m in range(ROW_TILES)]
+        FIRST_VALUE_STEP = len(steps) - ROW_TILES
+
+        def start_side(i):
+            if i < len(operands):
+                c, g, h = operands[i]
+                return [pass_through(w_raw[(c, g)], h, part) for part in range(2)]
+            if FIRST_VALUE_STEP <= i < len(steps):
+                return multiply(VALUES, i - FIRST_VALUE_STEP, side_pool, "side")
+            return None
+
+        def start_step(i):
+            if i < len(steps):
+                c, m = steps[i]
+                return multiply(c, m, acc_pool, "acc")
+            return None
+
+        acc = {0: start_step(0)}
+        side = {0: start_side(0)}
+        acc[1] = start_step(1)
+        grouped = {}
+        for i in range(len(steps)):
+            c, m = steps[i]
+            view, first = chunk_out[c]
+            if 1 <= i <= len(operands):
+                done_c, done_g, done_h = operands[i - 1]
+                quantise_w(grouped[i - 1], done_c, done_g, done_h)
+            inverse = inverse_rms(sum_squares(acc[i]))
+            if i < len(operands):
+                grouped[i] = new_grouped()
+                for part in range(2):
+                    nc.scalar.copy(
+                        out=grouped[i][:, part * HALF_BANK : (part + 1) * HALF_BANK, :].rearrange("p n t -> p (n t)"),
+                        in_=side[i][part][:],
                     )
+            elif side[i] is not None:
+                value_view, value_first = chunk_out[VALUES]
+                nc.scalar.dma_start(
+                    out=value_view[i - FIRST_VALUE_STEP, :, value_first : value_first + CHUNK],
+                    in_=copy_values(side[i])[:],
+                )
+            side[i + 1] = start_side(i + 1)
+            acc[i + 2] = start_step(i + 2)
+            result = norm_and_rope(acc[i], inverse, q_table if c < 2 else k_table, m)
+            nc.sync.dma_start(out=view[m, :, first : first + CHUNK], in_=result[:].rearrange("p j d -> p (j d)"))

@@ -315,8 +315,10 @@ def tile_gemmaattention_pa_kernel(
                 grouped[i] = new_grouped()
                 for part in range(2):
                     nc.scalar.copy(
-                        out=grouped[i][:, part * HALF_BANK : (part + 1) * HALF_BANK, :].rearrange("p n t -> p (n t)"),
-                        in_=side[i][part][:],
+                        out=grouped[i][:, part * HALF_BANK : (part + 1) * HALF_BANK, :]
+                        .rearrange("p n t -> p (n t)")
+                        .bitcast(F32),
+                        in_=side[i][part][:].bitcast(F32),
                     )
             elif side[i] is not None:
                 value_view, value_first = chunk_out[VALUES]

@@ -33,6 +33,7 @@ CHUNK_HEADS = CHUNK // HEAD
 X_PIECES = 4
 PIECE_TILES = ROW_TILES // X_PIECES
 PIECE_ROWS = PIECE_TILES * P
+GROUPED_BUFS = 4
 
 FLOPS = 2 * ROWS * HID * (Q_COLS + K_COLS + V_COLS)
 
@@ -55,13 +56,12 @@ def tile_gemmaattention_pa_kernel(
         stack.enter_context(tc.manual_schedule())
         keep = stack.enter_context(tc.tile_pool(name="keep", bufs=1))
         w_raw_pool = stack.enter_context(tc.tile_pool(name="w_raw", bufs=6))
-        w_grouped_pool = stack.enter_context(tc.tile_pool(name="w_grouped", bufs=4))
+        w_grouped_pool = stack.enter_context(tc.tile_pool(name="w_grouped", bufs=GROUPED_BUFS))
         products_pool = stack.enter_context(tc.tile_pool(name="products", bufs=3))
         result_pool = stack.enter_context(tc.tile_pool(name="result", bufs=4))
         squares_pool = stack.enter_context(tc.tile_pool(name="squares", bufs=4))
         stats_pool = stack.enter_context(tc.tile_pool(name="stats", bufs=6))
-        acc_pool = stack.enter_context(tc.psum_pool(name="acc", bufs=6))
-        side_pool = stack.enter_context(tc.psum_pool(name="side", bufs=2))
+        psum = stack.enter_context(tc.psum_pool(name="psum", bufs=1))
 
         identity = keep.tile([P, P], F32)
         identity_bf = keep.tile([P, P], BF16)
@@ -73,6 +73,21 @@ def tile_gemmaattention_pa_kernel(
         w_scales = keep.tile([P, PASSES, CHUNKS * CHUNK], U8, align_bytes=64)
         q_table = keep.tile([P, 2, ROW_TILES, HEAD], F32)
         k_table = keep.tile([P, 2, ROW_TILES, HEAD], F32)
+
+        steps = [(c, m) for c in range(VALUES) for m in range(ROW_TILES)]
+        operands = [(c, g, h) for c in range(1, CHUNKS) for g in range(PASSES) for h in range(2)]
+        halves = [(operand, part) for operand in operands for part in range(2)]
+
+        x_ready = set()
+        w_ready = set()
+        free_pairs = [0, 1, 2]
+        tensor_jobs = [("turn", i) for i in range(X_PIECES)] + [("step", i) for i in range(len(steps))]
+        pair_of = {}
+        banks_of = {}
+        w_raw = {}
+        grouped = {}
+        parts_written = {}
+        count = {"halves": 0, "values": 0}
 
         def load_x_piece(i):
             cols = slice(i * PIECE_TILES * HID, (i + 1) * PIECE_TILES * HID)
@@ -89,18 +104,15 @@ def tile_gemmaattention_pa_kernel(
                     "(p t) n -> p t n", t=PACK
                 ),
             )
-            return raw
+            w_raw[(c, g)] = raw
 
-        def quantise_x_piece(i):
+        def turn(i, banks):
             x_words = x_raw[:].bitcast(F32)
             words_per_row = HID // 2
             words_per_pass = K_PASS // 2
-            grouped = x_grouped_pool.tile([P, PASSES * PIECE_ROWS * PACK], BF16, align_bytes=64, tag="x_grouped")
-            grouped_words = grouped[:].bitcast(F32).rearrange("p (g s u) -> p g s u", g=PASSES, u=2)
             for local in range(PIECE_TILES):
                 m = i * PIECE_TILES + local
-                turned = acc_pool.tile([P, BANK], F32, tag="acc", name="turned_%d" % m)
-                turned_gus = turned[:].rearrange("p (g u s) -> p g u s", g=PASSES, u=2)
+                turned_gus = banks[local][:].rearrange("p (g u s) -> p g u s", g=PASSES, u=2)
                 for g in range(PASSES):
                     for u in range(2):
                         first = m * words_per_row + g * words_per_pass
@@ -109,30 +121,117 @@ def tile_gemmaattention_pa_kernel(
                             x_words[:, first + u : first + words_per_pass : 2],
                             identity[:],
                         )
+
+        def multiply(c, m, banks):
+            piece, local = divmod(m, PIECE_TILES)
+            for g in range(PASSES):
+                rows = slice(g * PIECE_ROWS + local * P, g * PIECE_ROWS + (local + 1) * P)
+                for h in range(2):
+                    cols = slice(c * CHUNK + h * BANK, c * CHUNK + (h + 1) * BANK)
+                    nc.tensor.matmul_mx(
+                        out=banks[h][:],
+                        lhsT=x_codes[:, piece, rows].bitcast(FP8X4),
+                        lhsT_scale=x_scales[:, piece, rows],
+                        rhs=w_codes[:, g, cols].bitcast(FP8X4),
+                        rhs_scale=w_scales[:, g, cols],
+                        start=(g == 0),
+                        stop=(g == PASSES - 1),
+                    )
+
+        def codes_written(c, m):
+            return (m // PIECE_TILES) in x_ready and all((c, g, h) in w_ready for g in range(PASSES) for h in range(2))
+
+        def pump():
+            while tensor_jobs and free_pairs:
+                job = tensor_jobs[0]
+                if job[0] == "step" and not codes_written(steps[job[1]][0], steps[job[1]][1]):
+                    return
+                pair = free_pairs[0]
+                tensor_jobs.remove(job)
+                free_pairs.remove(pair)
+                pair_of[job] = pair
+                banks = [
+                    psum.tile([P, BANK], F32, tag="pair%d%s" % (pair, x), name="%s_%d_%s" % (job[0], job[1], x))
+                    for x in ("a", "b")
+                ]
+                banks_of[job] = banks
+                if job[0] == "turn":
+                    turn(job[1], banks)
+                else:
+                    multiply(steps[job[1]][0], steps[job[1]][1], banks)
+
+        def release(job):
+            free_pairs.append(pair_of[job])
+            pump()
+
+        def copy_x_piece(i):
+            tile = x_grouped_pool.tile([P, PASSES * PIECE_ROWS * PACK], BF16, align_bytes=64, tag="x_grouped")
+            words = tile[:].bitcast(F32).rearrange("p (g s u) -> p g s u", g=PASSES, u=2)
+            for local in range(PIECE_TILES):
                 nc.scalar.copy(
-                    out=grouped_words[:, :, local * P : (local + 1) * P, :],
-                    in_=turned_gus.rearrange("p g u s -> p g s u"),
+                    out=words[:, :, local * P : (local + 1) * P, :],
+                    in_=banks_of[("turn", i)][local][:].rearrange("p (g u s) -> p g s u", g=PASSES, u=2),
                 )
-            nc.vector.quantize_mx(
-                out=x_codes[:, i, :].bitcast(FP8X4), scales=x_scales[:, i, :], in_=grouped[:]
-            )
+            release(("turn", i))
+            return tile
 
-        def new_grouped():
-            return w_grouped_pool.tile([P, BANK, PACK], BF16, align_bytes=64, tag="w_grouped", name="w_grouped")
+        def quantise_x_piece(i, tile):
+            nc.vector.quantize_mx(out=x_codes[:, i, :].bitcast(FP8X4), scales=x_scales[:, i, :], in_=tile[:])
+            x_ready.add(i)
+            pump()
 
-        def regroup_w(engine_copy, grouped, raw, h, first, count):
+        def grouped_tile(operand):
+            if operand not in grouped:
+                assert len(grouped) - len([o for o in grouped if o in w_ready]) < GROUPED_BUFS
+                grouped[operand] = w_grouped_pool.tile(
+                    [P, BANK, PACK], BF16, align_bytes=64, tag="w_grouped", name="w_grouped"
+                )
+                parts_written[operand] = 0
+            return grouped[operand]
+
+        def regroup_w(engine_copy, operand, first, width):
+            c, g, h = operand
             engine_copy(
-                out=grouped[:, first : first + count, :].rearrange("p (n i) t -> p n t i", i=4),
-                in_=raw[:, :, h * BANK + first : h * BANK + first + count].rearrange("p t (n i) -> p n t i", i=4),
+                out=grouped_tile(operand)[:, first : first + width, :].rearrange("p (n i) t -> p n t i", i=4),
+                in_=w_raw[(c, g)][:, :, h * BANK + first : h * BANK + first + width].rearrange(
+                    "p t (n i) -> p n t i", i=4
+                ),
             )
+            parts_written[operand] += width // HALF_BANK
 
-        def quantise_w(grouped, c, g, h):
+        def pass_through(operand, part):
+            c, g, h = operand
+            bank = psum.tile([P, 2 * BANK], BF16, tag="side_a", name="through")
+            for q in range(2):
+                first = h * BANK + part * HALF_BANK + q * P
+                nc.tensor.matmul(
+                    out=bank[:, q * BANK : (q + 1) * BANK].rearrange("p (n t) -> p n t", t=PACK),
+                    lhsT=identity_bf[:],
+                    rhs=w_raw[(c, g)][:, :, first : first + P].rearrange("p t n -> p n t"),
+                    start=True,
+                    stop=True,
+                )
+            return bank
+
+        def copy_through(operand, part, bank):
+            nc.scalar.copy(
+                out=grouped_tile(operand)[:, part * HALF_BANK : (part + 1) * HALF_BANK, :]
+                .rearrange("p n t -> p (n t)")
+                .bitcast(F32),
+                in_=bank[:].bitcast(F32),
+            )
+            parts_written[operand] += 1
+
+        def quantise_w(operand):
+            c, g, h = operand
             cols = slice(c * CHUNK + h * BANK, c * CHUNK + (h + 1) * BANK)
             nc.vector.quantize_mx(
                 out=w_codes[:, g, cols].bitcast(FP8X4),
                 scales=w_scales[:, g, cols],
-                in_=grouped[:].rearrange("p n t -> p (n t)"),
+                in_=grouped[operand][:].rearrange("p n t -> p (n t)"),
             )
+            w_ready.add(operand)
+            pump()
 
         def make_table(table, first):
             low, high = slice(0, HALF), slice(HALF, HEAD)
@@ -151,37 +250,6 @@ def tile_gemmaattention_pa_kernel(
                     op0=ALU.add,
                     op1=ALU.mult,
                 )
-
-        def pass_through(raw, h, part):
-            bank = side_pool.tile([P, 2 * BANK], BF16, tag="side", name="through")
-            for q in range(2):
-                first = h * BANK + part * HALF_BANK + q * P
-                nc.tensor.matmul(
-                    out=bank[:, q * BANK : (q + 1) * BANK].rearrange("p (n t) -> p n t", t=PACK),
-                    lhsT=identity_bf[:],
-                    rhs=raw[:, :, first : first + P].rearrange("p t n -> p n t"),
-                    start=True,
-                    stop=True,
-                )
-            return bank
-
-        def multiply(c, m, pool, tag):
-            banks = [pool.tile([P, BANK], F32, tag=tag, name="acc_%d_%d_%d" % (c, m, h)) for h in range(2)]
-            piece, local = divmod(m, PIECE_TILES)
-            for g in range(PASSES):
-                rows = slice(g * PIECE_ROWS + local * P, g * PIECE_ROWS + (local + 1) * P)
-                for h in range(2):
-                    cols = slice(c * CHUNK + h * BANK, c * CHUNK + (h + 1) * BANK)
-                    nc.tensor.matmul_mx(
-                        out=banks[h][:],
-                        lhsT=x_codes[:, piece, rows].bitcast(FP8X4),
-                        lhsT_scale=x_scales[:, piece, rows],
-                        rhs=w_codes[:, g, cols].bitcast(FP8X4),
-                        rhs_scale=w_scales[:, g, cols],
-                        start=(g == 0),
-                        stop=(g == PASSES - 1),
-                    )
-            return banks
 
         def head_in_banks(banks, j):
             heads_per_bank = BANK // HEAD
@@ -205,7 +273,7 @@ def tile_gemmaattention_pa_kernel(
             )
             return inverse
 
-        def norm_and_rope(banks, inverse, table, m):
+        def rope_products(banks, inverse, table, m):
             products = products_pool.tile([P, CHUNK_HEADS, 2, HEAD], F32, tag="products")
             for j in range(CHUNK_HEADS):
                 nc.vector.scalar_tensor_tensor(
@@ -216,18 +284,15 @@ def tile_gemmaattention_pa_kernel(
                     op0=ALU.mult,
                     op1=ALU.mult,
                 )
+            return products
+
+        def rope_sums(products):
             result = result_pool.tile([P, CHUNK_HEADS, HEAD], F32, tag="result")
             terms = products[:].rearrange("p j r (x i) -> p (j r) x i", x=2)
             nc.gpsimd.tensor_tensor(
                 out=result[:].rearrange("p j (r i) -> p (j r) i", r=2),
                 in0=terms[:, :, 0, :], in1=terms[:, :, 1, :], op=ALU.add,
             )
-            return result
-
-        def copy_values(banks):
-            result = values_pool.tile([P, CHUNK], F32, tag="values")
-            nc.scalar.copy(out=result[:, 0:BANK], in_=banks[0][:])
-            nc.scalar.copy(out=result[:, BANK:CHUNK], in_=banks[1][:])
             return result
 
         with tc.tile_pool(name="start", bufs=1) as start, tc.tile_pool(name="x_grouped", bufs=2) as x_grouped_pool:
@@ -239,19 +304,15 @@ def tile_gemmaattention_pa_kernel(
             weight_rows = start.tile([P, 2 * HEAD], BF16)
 
             nc.vector.memset(weight_rows[:], 0.0)
-            w_raw = {}
             nc.sync.dma_start(out=cos_raw[:], in_=cos_rows)
             nc.sync.dma_start(out=weight_rows[0:1, 0:HEAD], in_=q_norm_w.unsqueeze(0))
             nc.sync.dma_start(out=weight_rows[0:1, HEAD : 2 * HEAD], in_=k_norm_w.unsqueeze(0))
             nc.sync.dma_start(out=sin_raw[:], in_=sin_rows)
-            load_x_piece(0)
-            for g in range(PASSES):
-                w_raw[(0, g)] = load_w(0, g)
-            for i in range(1, X_PIECES):
+            for i in range(X_PIECES):
                 load_x_piece(i)
-            for c in (1, 2):
+            for c in range(VALUES):
                 for g in range(PASSES):
-                    w_raw[(c, g)] = load_w(c, g)
+                    load_w(c, g)
 
             make_identity(nc, identity[:])
             make_identity(nc, identity_bf[:])
@@ -259,74 +320,82 @@ def tile_gemmaattention_pa_kernel(
             nc.scalar.activation(out=warm[:], in_=eps[:], func=ACT.Abs_reciprocal_sqrt)
             nc.vector.memset(ones[:], 1.0)
             nc.vector.memset(minus_ones[:], -1.0)
-            spread_plus = side_pool.tile([P, BANK], F32, tag="side")
-            spread_minus = side_pool.tile([P, BANK], F32, tag="side")
+            spread_plus = psum.tile([P, BANK], F32, tag="side_a")
+            spread_minus = psum.tile([P, BANK], F32, tag="side_b")
             nc.tensor.matmul(out=spread_plus[:], lhsT=ones[:], rhs=weight_rows[:], start=True, stop=True)
             nc.tensor.matmul(out=spread_minus[:], lhsT=minus_ones[:], rhs=weight_rows[:], start=True, stop=True)
+            pump()
             make_table(q_table, 0)
+
+            for i in range(X_PIECES):
+                quantise_x_piece(i, copy_x_piece(i))
+            for g in range(PASSES):
+                regroup_w(nc.vector.tensor_copy, (0, g, 0), 0, BANK)
+                regroup_w(nc.scalar.copy, (0, g, 1), 0, BANK)
+                quantise_w((0, g, 0))
+                quantise_w((0, g, 1))
+            for g in range(PASSES):
+                load_w(VALUES, g)
             make_table(k_table, HEAD)
-
-            quantise_x_piece(0)
-            first_grouped = {}
-            for g in range(PASSES):
-                for h, engine_copy in ((0, nc.vector.tensor_copy), (1, nc.scalar.copy)):
-                    first_grouped[(g, h)] = new_grouped()
-                    regroup_w(engine_copy, first_grouped[(g, h)], w_raw[(0, g)], h, 0, BANK)
-            for g in range(PASSES):
-                for h in range(2):
-                    quantise_w(first_grouped[(g, h)], 0, g, h)
-            for g in range(PASSES):
-                w_raw[(CHUNKS - 1, g)] = load_w(CHUNKS - 1, g)
-            for i in range(1, X_PIECES):
-                quantise_x_piece(i)
-
         values_pool = stack.enter_context(tc.tile_pool(name="values", bufs=4))
 
-        operands = [(c, g, h) for c in range(1, CHUNKS) for g in range(PASSES) for h in range(2)]
-        steps = [(c, m) for c in range(VALUES) for m in range(ROW_TILES)]
-        FIRST_VALUE_STEP = len(steps) - ROW_TILES
+        def take_half():
+            item = halves[count["halves"]]
+            count["halves"] += 1
+            return item
 
-        def start_side(i):
-            if i < len(operands):
-                c, g, h = operands[i]
-                return [pass_through(w_raw[(c, g)], h, part) for part in range(2)]
-            if FIRST_VALUE_STEP <= i < len(steps):
-                return multiply(VALUES, i - FIRST_VALUE_STEP, side_pool, "side")
-            return None
+        def halves_left():
+            return count["halves"] < len(halves)
 
-        def start_step(i):
-            if i < len(steps):
-                c, m = steps[i]
-                return multiply(c, m, acc_pool, "acc")
-            return None
+        def start_through():
+            if not halves_left():
+                return None
+            operand, part = take_half()
+            return (operand, part, pass_through(operand, part))
 
-        acc = {0: start_step(0)}
-        side = {0: start_side(0)}
-        acc[1] = start_step(1)
-        grouped = {}
+        def start_values():
+            m = count["values"]
+            if m == ROW_TILES or halves_left() or not codes_written(VALUES, m):
+                return None
+            banks = [psum.tile([P, BANK], F32, tag="side_%s" % x, name="values_%d_%s" % (m, x)) for x in ("a", "b")]
+            multiply(VALUES, m, banks)
+            count["values"] += 1
+            return (m, banks)
+
+        def finish_values(m, banks):
+            result = values_pool.tile([P, CHUNK], F32, tag="values")
+            nc.scalar.copy(out=result[:, 0:BANK], in_=banks[0][:])
+            nc.scalar.copy(out=result[:, BANK:CHUNK], in_=banks[1][:])
+            view, first = chunk_out[VALUES]
+            nc.scalar.dma_start(out=view[m, :, first : first + CHUNK], in_=result[:])
+
+        operand, part = take_half()
+        regroup_w(nc.scalar.copy, operand, part * HALF_BANK, HALF_BANK)
+        through = start_through()
+        values = None
         for i in range(len(steps)):
             c, m = steps[i]
             view, first = chunk_out[c]
-            if 1 <= i <= len(operands):
-                done_c, done_g, done_h = operands[i - 1]
-                quantise_w(grouped[i - 1], done_c, done_g, done_h)
-            inverse = inverse_rms(sum_squares(acc[i]))
-            if i < len(operands):
-                grouped[i] = new_grouped()
-                for part in range(2):
-                    nc.scalar.copy(
-                        out=grouped[i][:, part * HALF_BANK : (part + 1) * HALF_BANK, :]
-                        .rearrange("p n t -> p (n t)")
-                        .bitcast(F32),
-                        in_=side[i][part][:].bitcast(F32),
-                    )
-            elif side[i] is not None:
-                value_view, value_first = chunk_out[VALUES]
-                nc.scalar.dma_start(
-                    out=value_view[i - FIRST_VALUE_STEP, :, value_first : value_first + CHUNK],
-                    in_=copy_values(side[i])[:],
-                )
-            side[i + 1] = start_side(i + 1)
-            acc[i + 2] = start_step(i + 2)
-            result = norm_and_rope(acc[i], inverse, q_table if c < 2 else k_table, m)
+            banks = banks_of[("step", i)]
+            whole = [o for o in operands if o not in w_ready and parts_written.get(o, 0) == 2]
+            if whole:
+                quantise_w(whole[0])
+            sums = sum_squares(banks)
+            if i % 2 == 1 and halves_left():
+                operand, part = take_half()
+                regroup_w(nc.scalar.copy, operand, part * HALF_BANK, HALF_BANK)
+            inverse = inverse_rms(sums)
+            if through is not None:
+                copy_through(through[0], through[1], through[2])
+                through = start_through()
+            if values is not None:
+                finish_values(values[0], values[1])
+            values = start_values() if through is None else None
+            products = rope_products(banks, inverse, q_table if c < 2 else k_table, m)
+            release(("step", i))
+            result = rope_sums(products)
             nc.sync.dma_start(out=view[m, :, first : first + CHUNK], in_=result[:].rearrange("p j d -> p (j d)"))
+        while values is not None:
+            finish_values(values[0], values[1])
+            values = start_values()
+        assert count["values"] == ROW_TILES and not tensor_jobs

@@ -34,6 +34,7 @@ X_PIECES = 4
 PIECE_TILES = ROW_TILES // X_PIECES
 PIECE_ROWS = PIECE_TILES * P
 GROUPED_BUFS = 4
+EARLY_STEPS = 8
 
 FLOPS = 2 * ROWS * HID * (Q_COLS + K_COLS + V_COLS)
 
@@ -233,23 +234,34 @@ def tile_gemmaattention_pa_kernel(
             w_ready.add(operand)
             pump()
 
-        def make_table(table, first):
+        def spread_weights(tag, first):
+            spread = psum.tile([P, BANK], F32, tag=tag, name="spread")
+            nc.tensor.matmul(
+                out=spread[:, 0:HEAD], lhsT=ones[:], rhs=weight_rows[:, first : first + HEAD], start=True, stop=True
+            )
+            nc.tensor.matmul(
+                out=spread[:, HEAD : HEAD + HALF], lhsT=minus_ones[:],
+                rhs=weight_rows[:, first + HALF : first + HEAD], start=True, stop=True,
+            )
+            return spread
+
+        def make_table_quarter(table, spread, quarter):
             low, high = slice(0, HALF), slice(HALF, HEAD)
-            for r, x_half, angles, angle_half, spread, one in (
-                (0, low, cos_raw, low, spread_plus, 1.0),
-                (0, high, sin_raw, low, spread_minus, -1.0),
-                (1, low, sin_raw, high, spread_plus, 1.0),
-                (1, high, cos_raw, high, spread_plus, 1.0),
-            ):
-                weight = spread[:, first + x_half.start : first + x_half.stop]
-                nc.vector.scalar_tensor_tensor(
-                    out=table[:, r, :, x_half],
-                    in0=weight.unsqueeze(1).to_broadcast([P, ROW_TILES, HALF]),
-                    scalar=one,
-                    in1=angles[:, :, angle_half],
-                    op0=ALU.add,
-                    op1=ALU.mult,
-                )
+            minus_high = slice(HEAD, HEAD + HALF)
+            r, x_half, angles, angle_half, weight_cols, one = (
+                (0, low, cos_raw, low, low, 1.0),
+                (0, high, sin_raw, low, minus_high, -1.0),
+                (1, low, sin_raw, high, low, 1.0),
+                (1, high, cos_raw, high, high, 1.0),
+            )[quarter]
+            nc.vector.scalar_tensor_tensor(
+                out=table[:, r, :, x_half],
+                in0=spread[:, weight_cols].unsqueeze(1).to_broadcast([P, ROW_TILES, HALF]),
+                scalar=one,
+                in1=angles[:, :, angle_half],
+                op0=ALU.add,
+                op1=ALU.mult,
+            )
 
         def head_in_banks(banks, j):
             heads_per_bank = BANK // HEAD
@@ -286,14 +298,80 @@ def tile_gemmaattention_pa_kernel(
                 )
             return products
 
-        def rope_sums(products):
+        def rope_sums(products, first_head, heads):
             result = result_pool.tile([P, CHUNK_HEADS, HEAD], F32, tag="result")
-            terms = products[:].rearrange("p j r (x i) -> p (j r) x i", x=2)
+            terms = products[:, first_head : first_head + heads, :, :].rearrange("p j r (x i) -> p (j r) x i", x=2)
             nc.gpsimd.tensor_tensor(
-                out=result[:].rearrange("p j (r i) -> p (j r) i", r=2),
+                out=result[:, 0:heads, :].rearrange("p j (r i) -> p (j r) i", r=2),
                 in0=terms[:, :, 0, :], in1=terms[:, :, 1, :], op=ALU.add,
             )
             return result
+
+        def take_half():
+            item = halves[count["halves"]]
+            count["halves"] += 1
+            return item
+
+        def halves_left():
+            return count["halves"] < len(halves)
+
+        def start_through():
+            if not halves_left():
+                return None
+            operand, part = take_half()
+            return (operand, part, pass_through(operand, part))
+
+        def start_values():
+            m = count["values"]
+            if m == ROW_TILES or halves_left() or not codes_written(VALUES, m):
+                return None
+            banks = [psum.tile([P, BANK], F32, tag="side_%s" % x, name="values_%d_%s" % (m, x)) for x in ("a", "b")]
+            multiply(VALUES, m, banks)
+            count["values"] += 1
+            return (m, banks)
+
+        def finish_values(m, banks, second_copy):
+            result = values_pool.tile([P, CHUNK], F32, tag="values")
+            nc.scalar.copy(out=result[:, 0:BANK], in_=banks[0][:])
+            second_copy(out=result[:, BANK:CHUNK], in_=banks[1][:])
+            view, first = chunk_out[VALUES]
+            nc.scalar.dma_start(out=view[m, :, first : first + CHUNK], in_=result[:])
+
+        state = {"through": None, "values": None}
+        inverse_of = {}
+
+        def run_step(i):
+            c, m = steps[i]
+            view, first = chunk_out[c]
+            banks = banks_of[("step", i)]
+            whole = [o for o in operands if o not in w_ready and parts_written.get(o, 0) == 2]
+            if whole:
+                quantise_w(whole[0])
+            elif k_quarters and i > 0:
+                make_table_quarter(k_table, k_spread, k_quarters[0])
+                k_quarters.remove(k_quarters[0])
+            if i + 1 < len(steps):
+                inverse_of[i + 1] = inverse_rms(sum_squares(banks_of[("step", i + 1)]))
+            if i % 2 == 1 and halves_left():
+                operand, part = take_half()
+                regroup_w(nc.scalar.copy, operand, part * HALF_BANK, HALF_BANK)
+            through = state["through"]
+            if through is not None:
+                copy_through(through[0], through[1], through[2])
+                state["through"] = start_through()
+            if state["values"] is not None:
+                finish_values(state["values"][0], state["values"][1], nc.scalar.copy)
+            state["values"] = start_values() if state["through"] is None else None
+            products = rope_products(banks, inverse_of[i], q_table if c < 2 else k_table, m)
+            release(("step", i))
+            pieces = 2 if i == len(steps) - 1 else 1
+            heads = CHUNK_HEADS // pieces
+            for piece in range(pieces):
+                result = rope_sums(products, piece * heads, heads)
+                nc.sync.dma_start(
+                    out=view[m, :, first + piece * heads * HEAD : first + (piece + 1) * heads * HEAD],
+                    in_=result[:, 0:heads, :].rearrange("p j d -> p (j d)"),
+                )
 
         with tc.tile_pool(name="start", bufs=1) as start, tc.tile_pool(name="x_grouped", bufs=2) as x_grouped_pool:
             x_raw = start.tile([P, ROW_TILES * HID], BF16)
@@ -320,12 +398,11 @@ def tile_gemmaattention_pa_kernel(
             nc.scalar.activation(out=warm[:], in_=eps[:], func=ACT.Abs_reciprocal_sqrt)
             nc.vector.memset(ones[:], 1.0)
             nc.vector.memset(minus_ones[:], -1.0)
-            spread_plus = psum.tile([P, BANK], F32, tag="side_a")
-            spread_minus = psum.tile([P, BANK], F32, tag="side_b")
-            nc.tensor.matmul(out=spread_plus[:], lhsT=ones[:], rhs=weight_rows[:], start=True, stop=True)
-            nc.tensor.matmul(out=spread_minus[:], lhsT=minus_ones[:], rhs=weight_rows[:], start=True, stop=True)
+            q_spread = spread_weights("side_a", 0)
+            k_spread = spread_weights("side_b", HEAD)
             pump()
-            make_table(q_table, 0)
+            for quarter in range(4):
+                make_table_quarter(q_table, q_spread, quarter)
 
             for i in range(X_PIECES):
                 quantise_x_piece(i, copy_x_piece(i))
@@ -336,66 +413,22 @@ def tile_gemmaattention_pa_kernel(
                 quantise_w((0, g, 1))
             for g in range(PASSES):
                 load_w(VALUES, g)
-            make_table(k_table, HEAD)
-        values_pool = stack.enter_context(tc.tile_pool(name="values", bufs=4))
+            k_quarters = [0, 1, 2, 3]
+            for quarter in (0, 1):
+                make_table_quarter(k_table, k_spread, quarter)
+                k_quarters.remove(quarter)
 
-        def take_half():
-            item = halves[count["halves"]]
-            count["halves"] += 1
-            return item
-
-        def halves_left():
-            return count["halves"] < len(halves)
-
-        def start_through():
-            if not halves_left():
-                return None
             operand, part = take_half()
-            return (operand, part, pass_through(operand, part))
-
-        def start_values():
-            m = count["values"]
-            if m == ROW_TILES or halves_left() or not codes_written(VALUES, m):
-                return None
-            banks = [psum.tile([P, BANK], F32, tag="side_%s" % x, name="values_%d_%s" % (m, x)) for x in ("a", "b")]
-            multiply(VALUES, m, banks)
-            count["values"] += 1
-            return (m, banks)
-
-        def finish_values(m, banks):
-            result = values_pool.tile([P, CHUNK], F32, tag="values")
-            nc.scalar.copy(out=result[:, 0:BANK], in_=banks[0][:])
-            nc.scalar.copy(out=result[:, BANK:CHUNK], in_=banks[1][:])
-            view, first = chunk_out[VALUES]
-            nc.scalar.dma_start(out=view[m, :, first : first + CHUNK], in_=result[:])
-
-        operand, part = take_half()
-        regroup_w(nc.scalar.copy, operand, part * HALF_BANK, HALF_BANK)
-        through = start_through()
-        values = None
-        for i in range(len(steps)):
-            c, m = steps[i]
-            view, first = chunk_out[c]
-            banks = banks_of[("step", i)]
-            whole = [o for o in operands if o not in w_ready and parts_written.get(o, 0) == 2]
-            if whole:
-                quantise_w(whole[0])
-            sums = sum_squares(banks)
-            if i % 2 == 1 and halves_left():
-                operand, part = take_half()
-                regroup_w(nc.scalar.copy, operand, part * HALF_BANK, HALF_BANK)
-            inverse = inverse_rms(sums)
-            if through is not None:
-                copy_through(through[0], through[1], through[2])
-                through = start_through()
-            if values is not None:
-                finish_values(values[0], values[1])
-            values = start_values() if through is None else None
-            products = rope_products(banks, inverse, q_table if c < 2 else k_table, m)
-            release(("step", i))
-            result = rope_sums(products)
-            nc.sync.dma_start(out=view[m, :, first : first + CHUNK], in_=result[:].rearrange("p j d -> p (j d)"))
-        while values is not None:
-            finish_values(values[0], values[1])
-            values = start_values()
+            regroup_w(nc.scalar.copy, operand, part * HALF_BANK, HALF_BANK)
+            state["through"] = start_through()
+            inverse_of[0] = inverse_rms(sum_squares(banks_of[("step", 0)]))
+            for i in range(EARLY_STEPS):
+                run_step(i)
+            assert not k_quarters
+        values_pool = stack.enter_context(tc.tile_pool(name="values", bufs=4))
+        for i in range(EARLY_STEPS, len(steps)):
+            run_step(i)
+        while state["values"] is not None:
+            finish_values(state["values"][0], state["values"][1], nc.vector.tensor_copy)
+            state["values"] = start_values()
         assert count["values"] == ROW_TILES and not tensor_jobs

@@ -34,7 +34,6 @@ X_PIECES = 4
 PIECE_TILES = ROW_TILES // X_PIECES
 PIECE_ROWS = PIECE_TILES * P
 GROUPED_BUFS = 4
-EARLY_STEPS = 8
 
 FLOPS = 2 * ROWS * HID * (Q_COLS + K_COLS + V_COLS)
 
@@ -88,7 +87,7 @@ def tile_gemmaattention_pa_kernel(
         w_raw = {}
         grouped = {}
         parts_written = {}
-        count = {"halves": 0, "values": 0}
+        count = {"halves": 0, "values": 0, "values_done": 0}
 
         def load_x_piece(i):
             cols = slice(i * PIECE_TILES * HID, (i + 1) * PIECE_TILES * HID)
@@ -166,7 +165,9 @@ def tile_gemmaattention_pa_kernel(
             pump()
 
         def copy_x_piece(i):
-            tile = x_grouped_pool.tile([P, PASSES * PIECE_ROWS * PACK], BF16, align_bytes=64, tag="x_grouped")
+            tile = x_grouped_pool.tile(
+                [P, PASSES * PIECE_ROWS * PACK], BF16, align_bytes=64, tag="x_grouped", name="x_grouped"
+            )
             words = tile[:].bitcast(F32).rearrange("p (g s u) -> p g s u", g=PASSES, u=2)
             for local in range(PIECE_TILES):
                 nc.scalar.copy(
@@ -322,34 +323,54 @@ def tile_gemmaattention_pa_kernel(
             return (operand, part, pass_through(operand, part))
 
         def start_values():
-            m = count["values"]
-            if m == ROW_TILES or halves_left() or not codes_written(VALUES, m):
-                return None
-            banks = [psum.tile([P, BANK], F32, tag="side_%s" % x, name="values_%d_%s" % (m, x)) for x in ("a", "b")]
-            multiply(VALUES, m, banks)
-            count["values"] += 1
-            return (m, banks)
+            while count["values"] < ROW_TILES and state["through"] is None and not halves_left():
+                m = count["values"]
+                if not codes_written(VALUES, m):
+                    return
+                if state["side_free"]:
+                    state["side_free"] = False
+                    pair = None
+                    tags = ("side_a", "side_b")
+                elif free_pairs and not tensor_jobs:
+                    pair = free_pairs[0]
+                    free_pairs.remove(pair)
+                    tags = ("pair%da" % pair, "pair%db" % pair)
+                else:
+                    return
+                banks = [psum.tile([P, BANK], F32, tag=tags[h], name="values_%d_%d" % (m, h)) for h in range(2)]
+                multiply(VALUES, m, banks)
+                value_banks[m] = (banks, pair)
+                count["values"] += 1
 
-        def finish_values(m, banks, second_copy):
+        def finish_values(second_copy):
+            m = count["values_done"]
+            banks, pair = value_banks[m]
             result = values_pool.tile([P, CHUNK], F32, tag="values")
             nc.scalar.copy(out=result[:, 0:BANK], in_=banks[0][:])
             second_copy(out=result[:, BANK:CHUNK], in_=banks[1][:])
             view, first = chunk_out[VALUES]
             nc.scalar.dma_start(out=view[m, :, first : first + CHUNK], in_=result[:])
+            count["values_done"] += 1
+            if pair is None:
+                state["side_free"] = True
+            else:
+                free_pairs.append(pair)
 
-        state = {"through": None, "values": None}
+        state = {"through": None, "side_free": True}
+        value_banks = {}
         inverse_of = {}
+        whole_since = {}
 
         def run_step(i):
             c, m = steps[i]
             view, first = chunk_out[c]
             banks = banks_of[("step", i)]
-            whole = [o for o in operands if o not in w_ready and parts_written.get(o, 0) == 2]
+            for o in operands:
+                if parts_written.get(o, 0) == 2 and o not in whole_since:
+                    whole_since[o] = i
+            whole = [o for o in operands if o not in w_ready and o in whole_since and whole_since[o] < i]
             if whole:
                 quantise_w(whole[0])
-            elif k_quarters and i > 0:
-                make_table_quarter(k_table, k_spread, k_quarters[0])
-                k_quarters.remove(k_quarters[0])
             if i + 1 < len(steps):
                 inverse_of[i + 1] = inverse_rms(sum_squares(banks_of[("step", i + 1)]))
             if i % 2 == 1 and halves_left():
@@ -359,11 +380,12 @@ def tile_gemmaattention_pa_kernel(
             if through is not None:
                 copy_through(through[0], through[1], through[2])
                 state["through"] = start_through()
-            if state["values"] is not None:
-                finish_values(state["values"][0], state["values"][1], nc.scalar.copy)
-            state["values"] = start_values() if state["through"] is None else None
+            if count["values_done"] < count["values"]:
+                finish_values(nc.scalar.copy)
+            start_values()
             products = rope_products(banks, inverse_of[i], q_table if c < 2 else k_table, m)
             release(("step", i))
+            start_values()
             pieces = 2 if i == len(steps) - 1 else 1
             heads = CHUNK_HEADS // pieces
             for piece in range(pieces):
@@ -373,13 +395,14 @@ def tile_gemmaattention_pa_kernel(
                     in_=result[:, 0:heads, :].rearrange("p j d -> p (j d)"),
                 )
 
-        with tc.tile_pool(name="start", bufs=1) as start, tc.tile_pool(name="x_grouped", bufs=2) as x_grouped_pool:
+        with tc.tile_pool(name="start", bufs=1) as start, tc.tile_pool(name="x_grouped", bufs=X_PIECES) as x_grouped_pool:
             x_raw = start.tile([P, ROW_TILES * HID], BF16)
             cos_raw = start.tile([P, ROW_TILES, HEAD], BF16)
             sin_raw = start.tile([P, ROW_TILES, HEAD], BF16)
             ones = start.tile([P, P], BF16)
             minus_ones = start.tile([P, P], BF16)
             weight_rows = start.tile([P, 2 * HEAD], BF16)
+            k_gain = start.tile([P, HEAD], F32)
 
             nc.vector.memset(weight_rows[:], 0.0)
             nc.sync.dma_start(out=cos_raw[:], in_=cos_rows)
@@ -401,34 +424,40 @@ def tile_gemmaattention_pa_kernel(
             q_spread = spread_weights("side_a", 0)
             k_spread = spread_weights("side_b", HEAD)
             pump()
+            nc.vector.tensor_scalar_add(out=k_gain[:], in0=k_spread[:, 0:HEAD], scalar1=1.0)
+            for x_half, angles in ((slice(HALF, HEAD), cos_raw), (slice(0, HALF), sin_raw)):
+                nc.gpsimd.tensor_tensor(
+                    out=k_table[:, 1, :, x_half],
+                    in0=angles[:, :, HALF:HEAD],
+                    in1=k_gain[:, x_half].unsqueeze(1).to_broadcast([P, ROW_TILES, HALF]),
+                    op=ALU.mult,
+                )
             for quarter in range(4):
                 make_table_quarter(q_table, q_spread, quarter)
 
-            for i in range(X_PIECES):
-                quantise_x_piece(i, copy_x_piece(i))
+            x_tiles = [copy_x_piece(i) for i in range(X_PIECES)]
+            for i in range(X_PIECES - 1):
+                quantise_x_piece(i, x_tiles[i])
             for g in range(PASSES):
                 regroup_w(nc.vector.tensor_copy, (0, g, 0), 0, BANK)
                 regroup_w(nc.scalar.copy, (0, g, 1), 0, BANK)
+                if g == 0:
+                    quantise_x_piece(X_PIECES - 1, x_tiles[X_PIECES - 1])
                 quantise_w((0, g, 0))
                 quantise_w((0, g, 1))
             for g in range(PASSES):
                 load_w(VALUES, g)
-            k_quarters = [0, 1, 2, 3]
             for quarter in (0, 1):
                 make_table_quarter(k_table, k_spread, quarter)
-                k_quarters.remove(quarter)
 
             operand, part = take_half()
             regroup_w(nc.scalar.copy, operand, part * HALF_BANK, HALF_BANK)
             state["through"] = start_through()
             inverse_of[0] = inverse_rms(sum_squares(banks_of[("step", 0)]))
-            for i in range(EARLY_STEPS):
-                run_step(i)
-            assert not k_quarters
         values_pool = stack.enter_context(tc.tile_pool(name="values", bufs=4))
-        for i in range(EARLY_STEPS, len(steps)):
+        for i in range(len(steps)):
             run_step(i)
-        while state["values"] is not None:
-            finish_values(state["values"][0], state["values"][1], nc.vector.tensor_copy)
-            state["values"] = start_values()
-        assert count["values"] == ROW_TILES and not tensor_jobs
+        while count["values_done"] < ROW_TILES:
+            finish_values(nc.vector.tensor_copy)
+            start_values()
+        assert not tensor_jobs

@@ -373,7 +373,7 @@ def tile_gemmaattention_pa_kernel(
                 quantise_w(whole[0])
             if i + 1 < len(steps):
                 inverse_of[i + 1] = inverse_rms(sum_squares(banks_of[("step", i + 1)]))
-            if i % 2 == 1 and halves_left():
+            if i % 2 == 0 and halves_left():
                 operand, part = take_half()
                 regroup_w(nc.scalar.copy, operand, part * HALF_BANK, HALF_BANK)
             through = state["through"]

@@ -207,9 +207,9 @@ def tile_gemmaattention_pa_kernel(
             for q in range(2):
                 first = h * BANK + part * HALF_BANK + q * P
                 nc.tensor.matmul(
-                    out=bank[:, q * BANK : (q + 1) * BANK].rearrange("p (n t) -> p n t", t=PACK),
+                    out=bank[:, q * BANK : (q + 1) * BANK].rearrange("p (n t) -> p t n", t=PACK),
                     lhsT=identity_bf[:],
-                    rhs=w_raw[(c, g)][:, :, first : first + P].rearrange("p t n -> p n t"),
+                    rhs=w_raw[(c, g)][:, :, first : first + P],
                     start=True,
                     stop=True,
                 )

@@ -33,6 +33,7 @@ CHUNK_HEADS = CHUNK // HEAD
 X_PIECES = 4
 PIECE_TILES = ROW_TILES // X_PIECES
 PIECE_ROWS = PIECE_TILES * P
+SIDES = ("side_a", "side_b")
 GROUPED_BUFS = 4
 
 FLOPS = 2 * ROWS * HID * (Q_COLS + K_COLS + V_COLS)
@@ -81,13 +82,18 @@ def tile_gemmaattention_pa_kernel(
         x_ready = set()
         w_ready = set()
         free_pairs = [0, 1, 2]
-        tensor_jobs = [("turn", i) for i in range(X_PIECES)] + [("step", i) for i in range(len(steps))]
+        tensor_jobs = [("turn", 0), ("turn", 1)]
+        later_jobs = [("turn", 2)]
+        for i in range(len(steps)):
+            if i == 2:
+                later_jobs.append(("turn", 3))
+            later_jobs.append(("step", i))
         pair_of = {}
         banks_of = {}
         w_raw = {}
         grouped = {}
         parts_written = {}
-        count = {"halves": 0, "values": 0, "values_done": 0}
+        count = {"halves": 0, "through": 0, "values": 0, "values_done": 0}
 
         def load_x_piece(i):
             cols = slice(i * PIECE_TILES * HID, (i + 1) * PIECE_TILES * HID)
@@ -201,9 +207,9 @@ def tile_gemmaattention_pa_kernel(
             )
             parts_written[operand] += width // HALF_BANK
 
-        def pass_through(operand, part):
+        def pass_through(operand, part, side):
             c, g, h = operand
-            bank = psum.tile([P, 2 * BANK], BF16, tag="side_a", name="through")
+            bank = psum.tile([P, 2 * BANK], BF16, tag=side, name="through")
             for q in range(2):
                 first = h * BANK + part * HALF_BANK + q * P
                 nc.tensor.matmul(
@@ -264,6 +270,15 @@ def tile_gemmaattention_pa_kernel(
                 op1=ALU.mult,
             )
 
+        def make_second_half(table, gain):
+            for x_half, angles in ((slice(HALF, HEAD), cos_raw), (slice(0, HALF), sin_raw)):
+                nc.gpsimd.tensor_tensor(
+                    out=table[:, 1, :, x_half],
+                    in0=angles[:, :, HALF:HEAD],
+                    in1=gain[:, x_half].unsqueeze(1).to_broadcast([P, ROW_TILES, HALF]),
+                    op=ALU.mult,
+                )
+
         def head_in_banks(banks, j):
             heads_per_bank = BANK // HEAD
             first = (j % heads_per_bank) * HEAD
@@ -317,20 +332,21 @@ def tile_gemmaattention_pa_kernel(
             return count["halves"] < len(halves)
 
         def start_through():
-            if not halves_left():
-                return None
-            operand, part = take_half()
-            return (operand, part, pass_through(operand, part))
+            if halves_left():
+                operand, part = take_half()
+                side = SIDES[count["through"] % len(SIDES)]
+                count["through"] += 1
+                state["through"].append((operand, part, pass_through(operand, part, side)))
 
         def start_values():
-            while count["values"] < ROW_TILES and state["through"] is None and not halves_left():
+            while count["values"] < ROW_TILES and not state["through"] and not halves_left():
                 m = count["values"]
                 if not codes_written(VALUES, m):
                     return
                 if state["side_free"]:
                     state["side_free"] = False
                     pair = None
-                    tags = ("side_a", "side_b")
+                    tags = SIDES
                 elif free_pairs and not tensor_jobs:
                     pair = free_pairs[0]
                     free_pairs.remove(pair)
@@ -356,7 +372,8 @@ def tile_gemmaattention_pa_kernel(
             else:
                 free_pairs.append(pair)
 
-        state = {"through": None, "side_free": True}
+        x_tiles = {}
+        state = {"through": [], "side_free": True}
         value_banks = {}
         inverse_of = {}
         whole_since = {}
@@ -365,21 +382,27 @@ def tile_gemmaattention_pa_kernel(
             c, m = steps[i]
             view, first = chunk_out[c]
             banks = banks_of[("step", i)]
+            if i == 2:
+                quantise_x_piece(3, x_tiles[3])
             for o in operands:
                 if parts_written.get(o, 0) == 2 and o not in whole_since:
                     whole_since[o] = i
             whole = [o for o in operands if o not in w_ready and o in whole_since and whole_since[o] < i]
-            if whole:
+            if whole and i != 2:
                 quantise_w(whole[0])
             if i + 1 < len(steps):
                 inverse_of[i + 1] = inverse_rms(sum_squares(banks_of[("step", i + 1)]))
-            if i % 2 == 0 and halves_left():
+            if i == 0 and True:
+                x_tiles[3] = copy_x_piece(3)
+            if i % 3 == 0 and halves_left():
                 operand, part = take_half()
                 regroup_w(nc.scalar.copy, operand, part * HALF_BANK, HALF_BANK)
-            through = state["through"]
-            if through is not None:
-                copy_through(through[0], through[1], through[2])
-                state["through"] = start_through()
+            for turn_of in range(1 + (i % 3 == 2)):
+                if state["through"]:
+                    through = state["through"][0]
+                    state["through"].remove(through)
+                    copy_through(through[0], through[1], through[2])
+                    start_through()
             if count["values_done"] < count["values"]:
                 finish_values(nc.scalar.copy)
             start_values()
@@ -402,16 +425,22 @@ def tile_gemmaattention_pa_kernel(
             ones = start.tile([P, P], BF16)
             minus_ones = start.tile([P, P], BF16)
             weight_rows = start.tile([P, 2 * HEAD], BF16)
+            q_gain = start.tile([P, HEAD], F32)
+            k_gain_early = start.tile([P, HEAD], F32)
             k_gain = start.tile([P, HEAD], F32)
 
             nc.vector.memset(weight_rows[:], 0.0)
             nc.sync.dma_start(out=cos_raw[:], in_=cos_rows)
             nc.sync.dma_start(out=weight_rows[0:1, 0:HEAD], in_=q_norm_w.unsqueeze(0))
             nc.sync.dma_start(out=weight_rows[0:1, HEAD : 2 * HEAD], in_=k_norm_w.unsqueeze(0))
+            load_x_piece(0)
             nc.sync.dma_start(out=sin_raw[:], in_=sin_rows)
-            for i in range(X_PIECES):
-                load_x_piece(i)
-            for c in range(VALUES):
+            load_x_piece(1)
+            for g in range(PASSES):
+                load_w(0, g)
+            load_x_piece(2)
+            load_x_piece(3)
+            for c in range(1, VALUES):
                 for g in range(PASSES):
                     load_w(c, g)
 
@@ -424,38 +453,45 @@ def tile_gemmaattention_pa_kernel(
             q_spread = spread_weights("side_a", 0)
             k_spread = spread_weights("side_b", HEAD)
             pump()
-            nc.vector.tensor_scalar_add(out=k_gain[:], in0=k_spread[:, 0:HEAD], scalar1=1.0)
-            for x_half, angles in ((slice(HALF, HEAD), cos_raw), (slice(0, HALF), sin_raw)):
-                nc.gpsimd.tensor_tensor(
-                    out=k_table[:, 1, :, x_half],
-                    in0=angles[:, :, HALF:HEAD],
-                    in1=k_gain[:, x_half].unsqueeze(1).to_broadcast([P, ROW_TILES, HALF]),
-                    op=ALU.mult,
-                )
-            for quarter in range(4):
-                make_table_quarter(q_table, q_spread, quarter)
+            nc.vector.tensor_scalar_add(out=q_gain[:], in0=q_spread[:, 0:HEAD], scalar1=1.0)
+            nc.vector.tensor_scalar_add(out=k_gain_early[:], in0=k_spread[:, 0:HEAD], scalar1=1.0)
+            make_second_half(q_table, q_gain)
+            for quarter in (0, 1):
+                for table, spread in ((q_table, q_spread), (k_table, k_spread)):
+                    make_table_quarter(table, spread, quarter)
 
-            x_tiles = [copy_x_piece(i) for i in range(X_PIECES)]
-            for i in range(X_PIECES - 1):
-                quantise_x_piece(i, x_tiles[i])
-            for g in range(PASSES):
-                regroup_w(nc.vector.tensor_copy, (0, g, 0), 0, BANK)
-                regroup_w(nc.scalar.copy, (0, g, 1), 0, BANK)
-                if g == 0:
-                    quantise_x_piece(X_PIECES - 1, x_tiles[X_PIECES - 1])
-                quantise_w((0, g, 0))
-                quantise_w((0, g, 1))
+            for i in range(2):
+                x_tiles[i] = copy_x_piece(i)
+            through_00 = pass_through((0, 0, 1), 0, "side_a")
+            regroup_w(nc.scalar.copy, (0, 0, 1), 1 * HALF_BANK, HALF_BANK)
+            copy_through((0, 0, 1), 0, through_00)
+            through_10 = pass_through((0, 1, 1), 0, "side_b")
+            regroup_w(nc.scalar.copy, (0, 1, 1), 1 * HALF_BANK, HALF_BANK)
+            copy_through((0, 1, 1), 0, through_10)
+            quantise_x_piece(0, x_tiles[0])
+            quantise_x_piece(1, x_tiles[1])
+            regroup_w(nc.vector.tensor_copy, (0, 0, 0), 0, BANK)
+            quantise_w((0, 0, 0))
+            regroup_w(nc.vector.tensor_copy, (0, 1, 0), 0, BANK)
+            quantise_w((0, 0, 1))
+            quantise_w((0, 1, 0))
+            quantise_w((0, 1, 1))
+            tensor_jobs.extend(later_jobs)
+            pump()
+            x_tiles[2] = copy_x_piece(2)
             for g in range(PASSES):
                 load_w(VALUES, g)
-            for quarter in (0, 1):
-                make_table_quarter(k_table, k_spread, quarter)
+            nc.vector.tensor_scalar_add(out=k_gain[:], in0=k_gain_early[:], scalar1=0.0)
+            make_second_half(k_table, k_gain)
+            quantise_x_piece(2, x_tiles[2])
 
-            operand, part = take_half()
-            regroup_w(nc.scalar.copy, operand, part * HALF_BANK, HALF_BANK)
-            state["through"] = start_through()
+            for side in SIDES:
+                start_through()
             inverse_of[0] = inverse_rms(sum_squares(banks_of[("step", 0)]))
+            for i in range(3):
+                run_step(i)
         values_pool = stack.enter_context(tc.tile_pool(name="values", bufs=4))
-        for i in range(len(steps)):
+        for i in range(3, len(steps)):
             run_step(i)
         while count["values_done"] < ROW_TILES:
             finish_values(nc.vector.tensor_copy)

@@ -394,10 +394,10 @@ def tile_gemmaattention_pa_kernel(
                 inverse_of[i + 1] = inverse_rms(sum_squares(banks_of[("step", i + 1)]))
             if i == 0 and True:
                 x_tiles[3] = copy_x_piece(3)
-            if i % 3 == 0 and halves_left():
+            if i % 2 == 0 and halves_left():
                 operand, part = take_half()
                 regroup_w(nc.scalar.copy, operand, part * HALF_BANK, HALF_BANK)
-            for turn_of in range(1 + (i % 3 == 2)):
+            for turn_of in range(1 + (i % 4 == 3)):
                 if state["through"]:
                     through = state["through"][0]
                     state["through"].remove(through)

@@ -76,7 +76,7 @@ def tile_gemmaattention_pa_kernel(
         k_table = keep.tile([P, 2, ROW_TILES, HEAD], F32)
 
         steps = [(c, m) for c in range(VALUES) for m in range(ROW_TILES)]
-        operands = [(c, g, h) for c in range(1, CHUNKS) for g in range(PASSES) for h in range(2)]
+        operands = [(c, g, h) for c in (1, 2, 3) for g in range(PASSES) for h in range(2)]
         halves = [(operand, part) for operand in operands for part in range(2)]
 
         x_ready = set()
@@ -314,10 +314,10 @@ def tile_gemmaattention_pa_kernel(
                 )
             return products
 
-        def rope_sums(products, first_head, heads):
+        def rope_sums(engine, products, first_head, heads):
             result = result_pool.tile([P, CHUNK_HEADS, HEAD], F32, tag="result")
             terms = products[:, first_head : first_head + heads, :, :].rearrange("p j r (x i) -> p (j r) x i", x=2)
-            nc.gpsimd.tensor_tensor(
+            engine.tensor_tensor(
                 out=result[:, 0:heads, :].rearrange("p j (r i) -> p (j r) i", r=2),
                 in0=terms[:, :, 0, :], in1=terms[:, :, 1, :], op=ALU.add,
             )
@@ -332,47 +332,72 @@ def tile_gemmaattention_pa_kernel(
             return count["halves"] < len(halves)
 
         def start_through():
-            if halves_left():
+            if halves_left() and free_sides:
+                if value_codes_written() and "side_a" not in free_sides:
+                    return
+                side = "side_a" if "side_a" in free_sides else "side_b"
+                free_sides.remove(side)
                 operand, part = take_half()
-                side = SIDES[count["through"] % len(SIDES)]
-                count["through"] += 1
-                state["through"].append((operand, part, pass_through(operand, part, side)))
+                state["through"].append((operand, part, pass_through(operand, part, side), side))
+
+        def value_codes_written():
+            return all((VALUES, g, h) in w_ready for g in range(PASSES) for h in range(2))
 
         def start_values():
-            while count["values"] < ROW_TILES and not state["through"] and not halves_left():
-                m = count["values"]
+            while count["values"] < 2 * ROW_TILES and value_codes_written():
+                m, h = divmod(count["values"], 2)
                 if not codes_written(VALUES, m):
                     return
-                if state["side_free"]:
-                    state["side_free"] = False
-                    pair = None
-                    tags = SIDES
-                elif free_pairs and not tensor_jobs:
+                pair = None
+                regrouping = halves_left() or state["through"]
+                if "side_b" in free_sides:
+                    tag = "side_b"
+                    free_sides.remove(tag)
+                elif "side_a" in free_sides and not regrouping:
+                    tag = "side_a"
+                    free_sides.remove(tag)
+                elif free_pairs and not tensor_jobs and not regrouping:
                     pair = free_pairs[0]
                     free_pairs.remove(pair)
-                    tags = ("pair%da" % pair, "pair%db" % pair)
+                    tag = "pair%da" % pair
                 else:
                     return
-                banks = [psum.tile([P, BANK], F32, tag=tags[h], name="values_%d_%d" % (m, h)) for h in range(2)]
-                multiply(VALUES, m, banks)
-                value_banks[m] = (banks, pair)
+                bank = psum.tile([P, BANK], F32, tag=tag, name="values_%d_%d" % (m, h))
+                piece, local = divmod(m, PIECE_TILES)
+                for g in range(PASSES):
+                    rows = slice(g * PIECE_ROWS + local * P, g * PIECE_ROWS + (local + 1) * P)
+                    cols = slice(VALUES * CHUNK + h * BANK, VALUES * CHUNK + (h + 1) * BANK)
+                    nc.tensor.matmul_mx(
+                        out=bank[:],
+                        lhsT=x_codes[:, piece, rows].bitcast(FP8X4),
+                        lhsT_scale=x_scales[:, piece, rows],
+                        rhs=w_codes[:, g, cols].bitcast(FP8X4),
+                        rhs_scale=w_scales[:, g, cols],
+                        start=(g == 0),
+                        stop=(g == PASSES - 1),
+                    )
+                value_banks[(m, h)] = (bank, pair, tag)
                 count["values"] += 1
 
-        def finish_values(second_copy):
-            m = count["values_done"]
-            banks, pair = value_banks[m]
-            result = values_pool.tile([P, CHUNK], F32, tag="values")
-            nc.scalar.copy(out=result[:, 0:BANK], in_=banks[0][:])
-            second_copy(out=result[:, BANK:CHUNK], in_=banks[1][:])
-            view, first = chunk_out[VALUES]
-            nc.scalar.dma_start(out=view[m, :, first : first + CHUNK], in_=result[:])
+        def finish_values(engine_copy):
+            m, h = divmod(count["values_done"], 2)
+            bank, pair, tag = value_banks[(m, h)]
+            if h == 0:
+                value_results[m] = values_pool.tile([P, CHUNK], F32, tag="values", name="values_out")
+            result = value_results[m]
+            engine_copy(out=result[:, h * BANK : (h + 1) * BANK], in_=bank[:])
+            if h == 1:
+                view, first = chunk_out[VALUES]
+                nc.scalar.dma_start(out=view[m, :, first : first + CHUNK], in_=result[:])
             count["values_done"] += 1
             if pair is None:
-                state["side_free"] = True
+                free_sides.append(tag)
             else:
                 free_pairs.append(pair)
 
+        value_results = {}
         x_tiles = {}
+        free_sides = ["side_a", "side_b"]
         state = {"through": [], "side_free": True}
         value_banks = {}
         inverse_of = {}
@@ -397,14 +422,18 @@ def tile_gemmaattention_pa_kernel(
             if i % 2 == 0 and halves_left():
                 operand, part = take_half()
                 regroup_w(nc.scalar.copy, operand, part * HALF_BANK, HALF_BANK)
-            for turn_of in range(1 + (i % 4 == 3)):
+            for turn_of in range(1 + (i % 2 and i > 2)):
                 if state["through"]:
                     through = state["through"][0]
                     state["through"].remove(through)
                     copy_through(through[0], through[1], through[2])
+                    free_sides.append(through[3])
                     start_through()
-            if count["values_done"] < count["values"]:
-                finish_values(nc.scalar.copy)
+            for turn_of in range(1 if halves_left() or state["through"] else 2):
+                if count["values_done"] < count["values"]:
+                    finish_values(nc.scalar.copy)
+                    if not (halves_left() or state["through"]):
+                        start_values()
             start_values()
             products = rope_products(banks, inverse_of[i], q_table if c < 2 else k_table, m)
             release(("step", i))
@@ -412,7 +441,8 @@ def tile_gemmaattention_pa_kernel(
             pieces = 2 if i == len(steps) - 1 else 1
             heads = CHUNK_HEADS // pieces
             for piece in range(pieces):
-                result = rope_sums(products, piece * heads, heads)
+                engine = nc.vector if i == len(steps) - 1 else nc.gpsimd
+                result = rope_sums(engine, products, piece * heads, heads)
                 nc.sync.dma_start(
                     out=view[m, :, first + piece * heads * HEAD : first + (piece + 1) * heads * HEAD],
                     in_=result[:, 0:heads, :].rearrange("p j d -> p (j d)"),
@@ -440,7 +470,7 @@ def tile_gemmaattention_pa_kernel(
                 load_w(0, g)
             load_x_piece(2)
             load_x_piece(3)
-            for c in range(1, VALUES):
+            for c in (1, 2):
                 for g in range(PASSES):
                     load_w(c, g)
 
@@ -480,7 +510,7 @@ def tile_gemmaattention_pa_kernel(
             pump()
             x_tiles[2] = copy_x_piece(2)
             for g in range(PASSES):
-                load_w(VALUES, g)
+                load_w(3, g)
             nc.vector.tensor_scalar_add(out=k_gain[:], in0=k_gain_early[:], scalar1=0.0)
             make_second_half(k_table, k_gain)
             quantise_x_piece(2, x_tiles[2])
@@ -493,7 +523,7 @@ def tile_gemmaattention_pa_kernel(
         values_pool = stack.enter_context(tc.tile_pool(name="values", bufs=4))
         for i in range(3, len(steps)):
             run_step(i)
-        while count["values_done"] < ROW_TILES:
-            finish_values(nc.vector.tensor_copy)
+        while count["values_done"] < 2 * ROW_TILES:
+            finish_values(nc.vector.tensor_copy if count["values_done"] % 2 else nc.scalar.copy)
             start_values()
         assert not tensor_jobs

from contextlib import ExitStack

import concourse.mybir as mybir
from concourse.masks import make_identity

F32 = mybir.dt.float32
BF16 = mybir.dt.bfloat16
U32 = mybir.dt.uint32
U8 = mybir.dt.uint8
FP8X4 = mybir.dt.float8_e4m3fn_x4
ACT = mybir.ActivationFunctionType
ALU = mybir.AluOpType

P = 128
ROWS = 1024
HID = 1024
HEAD = 256
HALF = HEAD // 2
Q_COLS = 2048
K_COLS = 1024
V_COLS = 1024
EPS = 1e-6

PACK = 4
K_PASS = P * PACK
PASSES = HID // K_PASS
ROW_TILES = ROWS // P
BANK = 512
HALF_BANK = BANK // 2
CHUNK = 2 * BANK
CHUNKS = (Q_COLS + K_COLS + V_COLS) // CHUNK
CHUNK_HEADS = CHUNK // HEAD
X_PIECES = 4
PIECE_TILES = ROW_TILES // X_PIECES
PIECE_ROWS = PIECE_TILES * P
SIDES = ("side_a", "side_b")
GROUPED_BUFS = 4

FLOPS = 2 * ROWS * HID * (Q_COLS + K_COLS + V_COLS)


def tile_gemmaattention_pa_kernel(
    tc, hidden_states, w_qkv, q_norm_w, k_norm_w, cos, sin, out_0, out_1, out_2
):
    nc = tc.nc

    x_rows = hidden_states.rearrange("(p m) k -> p m k", m=ROW_TILES)
    cos_rows = cos.rearrange("(p m) d -> p m d", m=ROW_TILES)
    sin_rows = sin.rearrange("(p m) d -> p m d", m=ROW_TILES)
    q_out = out_0.rearrange("(p m) h d -> m p (h d)", m=ROW_TILES)
    k_out = out_1.rearrange("(p m) h d -> m p (h d)", m=ROW_TILES)
    v_out = out_2.rearrange("(p m) h d -> m p (h d)", m=ROW_TILES)
    chunk_out = [(q_out, 0), (q_out, CHUNK), (k_out, 0), (v_out, 0)]
    VALUES = CHUNKS - 1

    with ExitStack() as stack:
        stack.enter_context(tc.manual_schedule())
        keep = stack.enter_context(tc.tile_pool(name="keep", bufs=1))
        w_raw_pool = stack.enter_context(tc.tile_pool(name="w_raw", bufs=6))
        w_grouped_pool = stack.enter_context(tc.tile_pool(name="w_grouped", bufs=GROUPED_BUFS))
        products_pool = stack.enter_context(tc.tile_pool(name="products", bufs=3))
        result_pool = stack.enter_context(tc.tile_pool(name="result", bufs=4))
        squares_pool = stack.enter_context(tc.tile_pool(name="squares", bufs=4))
        stats_pool = stack.enter_context(tc.tile_pool(name="stats", bufs=6))
        psum = stack.enter_context(tc.psum_pool(name="psum", bufs=1))

        identity = keep.tile([P, P], F32)
        identity_bf = keep.tile([P, P], BF16)
        eps = keep.tile([P, 1], F32)
        warm = keep.tile([P, 1], F32)
        x_codes = keep.tile([P, X_PIECES, PASSES * PIECE_ROWS], U32, align_bytes=64)
        x_scales = keep.tile([P, X_PIECES, PASSES * PIECE_ROWS], U8, align_bytes=64)
        w_codes = keep.tile([P, PASSES, CHUNKS * CHUNK], U32, align_bytes=64)
        w_scales = keep.tile([P, PASSES, CHUNKS * CHUNK], U8, align_bytes=64)
        q_table = keep.tile([P, 2, ROW_TILES, HEAD], F32)
        k_table = keep.tile([P, 2, ROW_TILES, HEAD], F32)

        steps = [(c, m) for c in range(VALUES) for m in range(ROW_TILES)]
        operands = [(c, g, h) for c in (1, 2, 3) for g in range(PASSES) for h in range(2)]
        halves = [(operand, part) for operand in operands for part in range(2)]

        x_ready = set()
        w_ready = set()
        free_pairs = [0, 1, 2]
        tensor_jobs = [("turn", 0), ("turn", 1)]
        later_jobs = [("turn", 2)]
        for i in range(len(steps)):
            if i == 2:
                later_jobs.append(("turn", 3))
            later_jobs.append(("step", i))
        pair_of = {}
        banks_of = {}
        w_raw = {}
        grouped = {}
        parts_written = {}
        count = {"halves": 0, "through": 0, "values": 0, "values_done": 0}

        def load_x_piece(i):
            cols = slice(i * PIECE_TILES * HID, (i + 1) * PIECE_TILES * HID)
            nc.sync.dma_start(
                out=x_raw[:, cols].rearrange("p (m k) -> p m k", m=PIECE_TILES),
                in_=x_rows[:, i * PIECE_TILES : (i + 1) * PIECE_TILES, :],
            )

        def load_w(c, g):
            raw = w_raw_pool.tile([P, PACK, CHUNK], BF16, tag="w_raw", name="w_raw_%d_%d" % (c, g))
            nc.sync.dma_start(
                out=raw[:],
                in_=w_qkv[g * K_PASS : (g + 1) * K_PASS, c * CHUNK : (c + 1) * CHUNK].rearrange(
                    "(p t) n -> p t n", t=PACK
                ),
            )
            w_raw[(c, g)] = raw

        def turn(i, banks):
            x_words = x_raw[:].bitcast(F32)
            words_per_row = HID // 2
            words_per_pass = K_PASS // 2
            for local in range(PIECE_TILES):
                m = i * PIECE_TILES + local
                turned_gus = banks[local][:].rearrange("p (g u s) -> p g u s", g=PASSES, u=2)
                for g in range(PASSES):
                    for u in range(2):
                        first = m * words_per_row + g * words_per_pass
                        nc.tensor.transpose(
                            turned_gus[:, g, u, :],
                            x_words[:, first + u : first + words_per_pass : 2],
                            identity[:],
                        )

        def multiply(c, m, banks):
            piece, local = divmod(m, PIECE_TILES)
            for g in range(PASSES):
                rows = slice(g * PIECE_ROWS + local * P, g * PIECE_ROWS + (local + 1) * P)
                for h in range(2):
                    cols = slice(c * CHUNK + h * BANK, c * CHUNK + (h + 1) * BANK)
                    nc.tensor.matmul_mx(
                        out=banks[h][:],
                        lhsT=x_codes[:, piece, rows].bitcast(FP8X4),
                        lhsT_scale=x_scales[:, piece, rows],
                        rhs=w_codes[:, g, cols].bitcast(FP8X4),
                        rhs_scale=w_scales[:, g, cols],
                        start=(g == 0),
                        stop=(g == PASSES - 1),
                    )

        def codes_written(c, m):
            return (m // PIECE_TILES) in x_ready and all((c, g, h) in w_ready for g in range(PASSES) for h in range(2))

        def pump():
            while tensor_jobs and free_pairs:
                job = tensor_jobs[0]
                if job[0] == "step" and not codes_written(steps[job[1]][0], steps[job[1]][1]):
                    return
                pair = free_pairs[0]
                tensor_jobs.remove(job)
                free_pairs.remove(pair)
                pair_of[job] = pair
                banks = [
                    psum.tile([P, BANK], F32, tag="pair%d%s" % (pair, x), name="%s_%d_%s" % (job[0], job[1], x))
                    for x in ("a", "b")
                ]
                banks_of[job] = banks
                if job[0] == "turn":
                    turn(job[1], banks)
                else:
                    multiply(steps[job[1]][0], steps[job[1]][1], banks)

        def release(job):
            free_pairs.append(pair_of[job])
            pump()

        def copy_x_piece(i):
            tile = x_grouped_pool.tile(
                [P, PASSES * PIECE_ROWS * PACK], BF16, align_bytes=64, tag="x_grouped", name="x_grouped"
            )
            words = tile[:].bitcast(F32).rearrange("p (g s u) -> p g s u", g=PASSES, u=2)
            for local in range(PIECE_TILES):
                nc.scalar.copy(
                    out=words[:, :, local * P : (local + 1) * P, :],
                    in_=banks_of[("turn", i)][local][:].rearrange("p (g u s) -> p g s u", g=PASSES, u=2),
                )
            release(("turn", i))
            return tile

        def quantise_x_piece(i, tile):
            nc.vector.quantize_mx(out=x_codes[:, i, :].bitcast(FP8X4), scales=x_scales[:, i, :], in_=tile[:])
            x_ready.add(i)
            pump()

        def grouped_tile(operand):
            if operand not in grouped:
                assert len(grouped) - len([o for o in grouped if o in w_ready]) < GROUPED_BUFS
                grouped[operand] = w_grouped_pool.tile(
                    [P, BANK, PACK], BF16, align_bytes=64, tag="w_grouped", name="w_grouped"
                )
                parts_written[operand] = 0
            return grouped[operand]

        def regroup_w(engine_copy, operand, first, width):
            c, g, h = operand
            engine_copy(
                out=grouped_tile(operand)[:, first : first + width, :].rearrange("p (n i) t -> p n t i", i=4),
                in_=w_raw[(c, g)][:, :, h * BANK + first : h * BANK + first + width].rearrange(
                    "p t (n i) -> p n t i", i=4
                ),
            )
            parts_written[operand] += width // HALF_BANK

        def pass_through(operand, part, side):
            c, g, h = operand
            bank = psum.tile([P, 2 * BANK], BF16, tag=side, name="through")
            for q in range(2):
                first = h * BANK + part * HALF_BANK + q * P
                nc.tensor.matmul(
                    out=bank[:, q * BANK : (q + 1) * BANK].rearrange("p (n t) -> p t n", t=PACK),
                    lhsT=identity_bf[:],
                    rhs=w_raw[(c, g)][:, :, first : first + P],
                    start=True,
                    stop=True,
                )
            return bank

        def copy_through(operand, part, bank):
            nc.scalar.copy(
                out=grouped_tile(operand)[:, part * HALF_BANK : (part + 1) * HALF_BANK, :]
                .rearrange("p n t -> p (n t)")
                .bitcast(F32),
                in_=bank[:].bitcast(F32),
            )
            parts_written[operand] += 1

        def quantise_w(operand):
            c, g, h = operand
            cols = slice(c * CHUNK + h * BANK, c * CHUNK + (h + 1) * BANK)
            nc.vector.quantize_mx(
                out=w_codes[:, g, cols].bitcast(FP8X4),
                scales=w_scales[:, g, cols],
                in_=grouped[operand][:].rearrange("p n t -> p (n t)"),
            )
            w_ready.add(operand)
            pump()

        def spread_weights(tag, first):
            spread = psum.tile([P, BANK], F32, tag=tag, name="spread")
            nc.tensor.matmul(
                out=spread[:, 0:HEAD], lhsT=ones[:], rhs=weight_rows[:, first : first + HEAD], start=True, stop=True
            )
            nc.tensor.matmul(
                out=spread[:, HEAD : HEAD + HALF], lhsT=minus_ones[:],
                rhs=weight_rows[:, first + HALF : first + HEAD], start=True, stop=True,
            )
            return spread

        def make_table_quarter(table, spread, quarter):
            low, high = slice(0, HALF), slice(HALF, HEAD)
            minus_high = slice(HEAD, HEAD + HALF)
            r, x_half, angles, angle_half, weight_cols, one = (
                (0, low, cos_raw, low, low, 1.0),
                (0, high, sin_raw, low, minus_high, -1.0),
                (1, low, sin_raw, high, low, 1.0),
                (1, high, cos_raw, high, high, 1.0),
            )[quarter]
            nc.vector.scalar_tensor_tensor(
                out=table[:, r, :, x_half],
                in0=spread[:, weight_cols].unsqueeze(1).to_broadcast([P, ROW_TILES, HALF]),
                scalar=one,
                in1=angles[:, :, angle_half],
                op0=ALU.add,
                op1=ALU.mult,
            )

        def make_second_half(table, gain):
            for x_half, angles in ((slice(HALF, HEAD), cos_raw), (slice(0, HALF), sin_raw)):
                nc.gpsimd.tensor_tensor(
                    out=table[:, 1, :, x_half],
                    in0=angles[:, :, HALF:HEAD],
                    in1=gain[:, x_half].unsqueeze(1).to_broadcast([P, ROW_TILES, HALF]),
                    op=ALU.mult,
                )

        def head_in_banks(banks, j):
            heads_per_bank = BANK // HEAD
            first = (j % heads_per_bank) * HEAD
            return banks[j // heads_per_bank][:, first : first + HEAD]

        def sum_squares(banks):
            sums = stats_pool.tile([P, CHUNK_HEADS], F32, tag="sums")
            for j in range(CHUNK_HEADS):
                squares = squares_pool.tile([P, HEAD], BF16, tag="squares")
                nc.scalar.activation(
                    out=squares[:], in_=head_in_banks(banks, j), func=ACT.Square,
                    accum_out=sums[:, j : j + 1],
                )
            return sums

        def inverse_rms(sums):
            inverse = stats_pool.tile([P, CHUNK_HEADS], F32, tag="inverse")
            nc.scalar.activation(
                out=inverse[:], in_=sums[:], func=ACT.Abs_reciprocal_sqrt, scale=1.0 / HEAD, bias=eps[:, 0:1]
            )
            return inverse

        def rope_products(banks, inverse, table, m):
            products = products_pool.tile([P, CHUNK_HEADS, 2, HEAD], F32, tag="products")
            for j in range(CHUNK_HEADS):
                nc.vector.scalar_tensor_tensor(
                    out=products[:, j, :, :],
                    in0=head_in_banks(banks, j).unsqueeze(1).to_broadcast([P, 2, HEAD]),
                    scalar=inverse[:, j : j + 1],
                    in1=table[:, :, m, :],
                    op0=ALU.mult,
                    op1=ALU.mult,
                )
            return products

        def rope_sums(engine, products, first_head, heads):
            result = result_pool.tile([P, CHUNK_HEADS, HEAD], F32, tag="result")
            terms = products[:, first_head : first_head + heads, :, :].rearrange("p j r (x i) -> p (j r) x i", x=2)
            engine.tensor_tensor(
                out=result[:, 0:heads, :].rearrange("p j (r i) -> p (j r) i", r=2),
                in0=terms[:, :, 0, :], in1=terms[:, :, 1, :], op=ALU.add,
            )
            return result

        def take_half():
            item = halves[count["halves"]]
            count["halves"] += 1
            return item

        def halves_left():
            return count["halves"] < len(halves)

        def start_through():
            if halves_left() and free_sides:
                if value_codes_written() and "side_a" not in free_sides:
                    return
                side = "side_a" if "side_a" in free_sides else "side_b"
                free_sides.remove(side)
                operand, part = take_half()
                state["through"].append((operand, part, pass_through(operand, part, side), side))

        def value_codes_written():
            return all((VALUES, g, h) in w_ready for g in range(PASSES) for h in range(2))

        def start_values():
            while count["values"] < 2 * ROW_TILES and value_codes_written():
                m, h = divmod(count["values"], 2)
                if not codes_written(VALUES, m):
                    return
                pair = None
                regrouping = halves_left() or state["through"]
                if "side_b" in free_sides:
                    tag = "side_b"
                    free_sides.remove(tag)
                elif "side_a" in free_sides and not regrouping:
                    tag = "side_a"
                    free_sides.remove(tag)
                elif free_pairs and not tensor_jobs and not regrouping:
                    pair = free_pairs[0]
                    free_pairs.remove(pair)
                    tag = "pair%da" % pair
                else:
                    return
                bank = psum.tile([P, BANK], F32, tag=tag, name="values_%d_%d" % (m, h))
                piece, local = divmod(m, PIECE_TILES)
                for g in range(PASSES):
                    rows = slice(g * PIECE_ROWS + local * P, g * PIECE_ROWS + (local + 1) * P)
                    cols = slice(VALUES * CHUNK + h * BANK, VALUES * CHUNK + (h + 1) * BANK)
                    nc.tensor.matmul_mx(
                        out=bank[:],
                        lhsT=x_codes[:, piece, rows].bitcast(FP8X4),
                        lhsT_scale=x_scales[:, piece, rows],
                        rhs=w_codes[:, g, cols].bitcast(FP8X4),
                        rhs_scale=w_scales[:, g, cols],
                        start=(g == 0),
                        stop=(g == PASSES - 1),
                    )
                value_banks[(m, h)] = (bank, pair, tag)
                count["values"] += 1

        def finish_values(engine_copy):
            m, h = divmod(count["values_done"], 2)
            bank, pair, tag = value_banks[(m, h)]
            if h == 0:
                value_results[m] = values_pool.tile([P, CHUNK], F32, tag="values", name="values_out")
            result = value_results[m]
            engine_copy(out=result[:, h * BANK : (h + 1) * BANK], in_=bank[:])
            if h == 1:
                view, first = chunk_out[VALUES]
                nc.scalar.dma_start(out=view[m, :, first : first + CHUNK], in_=result[:])
            count["values_done"] += 1
            if pair is None:
                free_sides.append(tag)
            else:
                free_pairs.append(pair)

        value_results = {}
        x_tiles = {}
        free_sides = ["side_a", "side_b"]
        state = {"through": [], "side_free": True}
        value_banks = {}
        inverse_of = {}
        whole_since = {}

        def run_step(i):
            c, m = steps[i]
            view, first = chunk_out[c]
            banks = banks_of[("step", i)]
            if i == 2:
                quantise_x_piece(3, x_tiles[3])
            for o in operands:
                if parts_written.get(o, 0) == 2 and o not in whole_since:
                    whole_since[o] = i
            whole = [o for o in operands if o not in w_ready and o in whole_since and whole_since[o] < i]
            if whole and i != 2:
                quantise_w(whole[0])
            if i + 1 < len(steps):
                inverse_of[i + 1] = inverse_rms(sum_squares(banks_of[("step", i + 1)]))
            if i == 0 and True:
                x_tiles[3] = copy_x_piece(3)
            if i % 2 == 0 and halves_left():
                operand, part = take_half()
                regroup_w(nc.scalar.copy, operand, part * HALF_BANK, HALF_BANK)
            for turn_of in range(1 + (i % 2 and i > 2)):
                if state["through"]:
                    through = state["through"][0]
                    state["through"].remove(through)
                    copy_through(through[0], through[1], through[2])
                    free_sides.append(through[3])
                    start_through()
            for turn_of in range(1 if halves_left() or state["through"] else 2):
                if count["values_done"] < count["values"]:
                    finish_values(nc.scalar.copy)
                    if not (halves_left() or state["through"]):
                        start_values()
            start_values()
            products = rope_products(banks, inverse_of[i], q_table if c < 2 else k_table, m)
            release(("step", i))
            start_values()
            pieces = 2 if i == len(steps) - 1 else 1
            heads = CHUNK_HEADS // pieces
            for piece in range(pieces):
                engine = nc.vector if i == len(steps) - 1 else nc.gpsimd
                result = rope_sums(engine, products, piece * heads, heads)
                nc.sync.dma_start(
                    out=view[m, :, first + piece * heads * HEAD : first + (piece + 1) * heads * HEAD],
                    in_=result[:, 0:heads, :].rearrange("p j d -> p (j d)"),
                )

        with tc.tile_pool(name="start", bufs=1) as start, tc.tile_pool(name="x_grouped", bufs=X_PIECES) as x_grouped_pool:
            x_raw = start.tile([P, ROW_TILES * HID], BF16)
            cos_raw = start.tile([P, ROW_TILES, HEAD], BF16)
            sin_raw = start.tile([P, ROW_TILES, HEAD], BF16)
            ones = start.tile([P, P], BF16)
            minus_ones = start.tile([P, P], BF16)
            weight_rows = start.tile([P, 2 * HEAD], BF16)
            q_gain = start.tile([P, HEAD], F32)
            k_gain_early = start.tile([P, HEAD], F32)
            k_gain = start.tile([P, HEAD], F32)

            nc.vector.memset(weight_rows[:], 0.0)
            nc.sync.dma_start(out=cos_raw[:], in_=cos_rows)
            nc.sync.dma_start(out=weight_rows[0:1, 0:HEAD], in_=q_norm_w.unsqueeze(0))
            nc.sync.dma_start(out=weight_rows[0:1, HEAD : 2 * HEAD], in_=k_norm_w.unsqueeze(0))
            load_x_piece(0)
            nc.sync.dma_start(out=sin_raw[:], in_=sin_rows)
            load_x_piece(1)
            for g in range(PASSES):
                load_w(0, g)
            load_x_piece(2)
            load_x_piece(3)
            for c in (1, 2):
                for g in range(PASSES):
                    load_w(c, g)

            make_identity(nc, identity[:])
            make_identity(nc, identity_bf[:])
            nc.vector.memset(eps[:], EPS)
            nc.scalar.activation(out=warm[:], in_=eps[:], func=ACT.Abs_reciprocal_sqrt)
            nc.vector.memset(ones[:], 1.0)
            nc.vector.memset(minus_ones[:], -1.0)
            q_spread = spread_weights("side_a", 0)
            k_spread = spread_weights("side_b", HEAD)
            pump()
            nc.vector.tensor_scalar_add(out=q_gain[:], in0=q_spread[:, 0:HEAD], scalar1=1.0)
            nc.vector.tensor_scalar_add(out=k_gain_early[:], in0=k_spread[:, 0:HEAD], scalar1=1.0)
            make_second_half(q_table, q_gain)
            for quarter in (0, 1):
                for table, spread in ((q_table, q_spread), (k_table, k_spread)):
                    make_table_quarter(table, spread, quarter)

            for i in range(2):
                x_tiles[i] = copy_x_piece(i)
            through_00 = pass_through((0, 0, 1), 0, "side_a")
            regroup_w(nc.scalar.copy, (0, 0, 1), 1 * HALF_BANK, HALF_BANK)
            copy_through((0, 0, 1), 0, through_00)
            through_10 = pass_through((0, 1, 1), 0, "side_b")
            regroup_w(nc.scalar.copy, (0, 1, 1), 1 * HALF_BANK, HALF_BANK)
            copy_through((0, 1, 1), 0, through_10)
            quantise_x_piece(0, x_tiles[0])
            quantise_x_piece(1, x_tiles[1])
            regroup_w(nc.vector.tensor_copy, (0, 0, 0), 0, BANK)
            quantise_w((0, 0, 0))
            regroup_w(nc.vector.tensor_copy, (0, 1, 0), 0, BANK)
            quantise_w((0, 0, 1))
            quantise_w((0, 1, 0))
            quantise_w((0, 1, 1))
            tensor_jobs.extend(later_jobs)
            pump()
            x_tiles[2] = copy_x_piece(2)
            for g in range(PASSES):
                load_w(3, g)
            nc.vector.tensor_scalar_add(out=k_gain[:], in0=k_gain_early[:], scalar1=0.0)
            make_second_half(k_table, k_gain)
            quantise_x_piece(2, x_tiles[2])

            for side in SIDES:
                start_through()
            inverse_of[0] = inverse_rms(sum_squares(banks_of[("step", 0)]))
            for i in range(3):
                run_step(i)
        values_pool = stack.enter_context(tc.tile_pool(name="values", bufs=4))
        for i in range(3, len(steps)):
            run_step(i)
        while count["values_done"] < 2 * ROW_TILES:
            finish_values(nc.vector.tensor_copy if count["values_done"] % 2 else nc.scalar.copy)
            start_values()
        assert not tensor_jobs
